import numpy as np
import ml_dtypes


def mxq(x, axis, fmt="e4m3"):
    dtype, down = {"e4m3": (ml_dtypes.float8_e4m3fn, 7), "e5m2": (ml_dtypes.float8_e5m2, 14)}[fmt]
    v = np.moveaxis(np.asarray(x, np.float32).astype(ml_dtypes.bfloat16).astype(np.float64), axis, -1)
    blocks = v.reshape(v.shape[:-1] + (-1, 32))
    amax = np.abs(blocks).max(-1, keepdims=True)
    byte = np.maximum(np.where(amax > 0, np.frexp(amax)[1] - 1 + 127, 0) - down, 1)
    scale = np.exp2(byte - 127.0)
    codes = (blocks / scale).astype(np.float32).astype(dtype).astype(np.float64)
    return np.moveaxis((codes * scale).reshape(v.shape), -1, axis)


WIDE = False


def mx_kscale(k):
    if not WIDE:
        return np.ones(k)
    levels = np.array([10, -10, 5, -5, 0])
    a = np.random.permutation(np.resize(levels, k // 512 * 4)).reshape(k // 512, 4)
    idx = np.arange(k)
    return np.exp2(a[idx // 512, idx % 128 // 32])


BF16 = ml_dtypes.bfloat16


def bf(x):
    return np.asarray(x, np.float32).astype(BF16)


def f64(x):
    return np.asarray(x).astype(np.float64)


B, T, D_IN, D_OUT, GRID_SIZE, SPLINE_ORDER, R = 6, 512, 64, 512, 5, 3, 2
NUM_GRIDS = GRID_SIZE + SPLINE_ORDER
K = D_IN * NUM_GRIDS
GRID_MIN, GRID_MAX = -1.5, 1.5
STEP = (GRID_MAX - GRID_MIN) / GRID_SIZE
EPS = 1e-5


def b_splines(x, grid):
    xg = x[..., None]
    bases = ((xg >= grid[:-1]) & (xg < grid[1:])).astype(np.float64)
    for k in range(1, SPLINE_ORDER + 1):
        bases = ((xg - grid[:-(k + 1)]) / (grid[k:-1] - grid[:-(k + 1)]) * bases[..., :-1]
                 + (grid[k + 1:] - xg) / (grid[k + 1:] - grid[1:-k]) * bases[..., 1:])
    return bases


def setup_inputs():
    row = np.exp(-4.6 * np.random.random_sample((R, T, 1)))
    f = mx_kscale(K)[::NUM_GRIDS]
    f = f / f.min()
    far = f > 1.0
    knots = np.arange(-SPLINE_ORDER, GRID_SIZE + SPLINE_ORDER + 1) * STEP + GRID_MIN
    grid = bf(knots + 0.1 * STEP * np.random.standard_normal(knots.shape))
    t = f64(grid)
    vol = np.prod(t[1:SPLINE_ORDER + 1] - t[0])
    lb_far = f64(bf(t[0] + np.maximum((vol / f) ** (1.0 / SPLINE_ORDER), 0.01)))
    gap = lb_far - t[0]
    return {"x": bf(np.random.standard_normal((R, T, D_IN)) * row),
            "ln_w": bf((1.0 + 0.1 * np.random.standard_normal(D_IN)) * np.where(far, 0.25 * gap, 1.0)),
            "ln_b": bf(np.where(far, lb_far, 0.1 * np.random.standard_normal(D_IN))),
            "spline_weight": bf(np.random.standard_normal((D_OUT, K)) / np.sqrt(D_IN) * np.repeat(np.where(far, 0.5 * vol / gap ** SPLINE_ORDER, 1.0), NUM_GRIDS)),
            "grid_bs": grid}


def reference(x, ln_w, ln_b, spline_weight, grid_bs):
    x = f64(x)
    mu = x.mean(-1, keepdims=True)
    var = x.var(-1, keepdims=True)
    xn = (x - mu) / np.sqrt(var + EPS) * f64(ln_w) + f64(ln_b)
    basis = b_splines(xn, f64(grid_bs)).reshape(R * T, K)
    y = mxq(basis, 1, "e4m3") @ mxq(f64(spline_weight), 1, "e4m3").T
    return y.reshape(R, T, D_OUT)

@@ -1,0 +1,244 @@
+from contextlib import ExitStack
+
+import concourse.mybir as mybir
+from concourse.masks import make_identity
+
+FLOPS = 2 * 1024 * 512 * 512
+
+BF16 = mybir.dt.bfloat16
+F32 = mybir.dt.float32
+U32 = mybir.dt.uint32
+U8 = mybir.dt.uint8
+FP8X4 = mybir.dt.float8_e4m3fn_x4
+ALU = mybir.AluOpType
+ACT = mybir.ActivationFunctionType
+
+P = 128
+PACK = 4
+FEATURES = 64
+OUTS = 512
+K = 512
+EPS = 1e-5
+GROUPS = 8
+CHUNK_GROUPS = 4
+CHUNKS = GROUPS // CHUNK_GROUPS
+CHUNK = CHUNK_GROUPS * P
+KNOTS = PACK + 4
+CUBES = PACK + 1
+FIRST_FALL = KNOTS - CUBES
+
+
+def tile_fc_kanlayer_pb_s_kernel(tc, x, ln_w, ln_b, spline_weight, grid_bs, out):
+    nc = tc.nc
+    with ExitStack() as ctx:
+        keep = ctx.enter_context(tc.tile_pool(name="keep", bufs=1))
+        work = ctx.enter_context(tc.tile_pool(name="work", bufs=2))
+        psum_z = ctx.enter_context(tc.psum_pool(name="psum_z", bufs=2))
+        psum_w = ctx.enter_context(tc.psum_pool(name="psum_w", bufs=2))
+        psum_out = ctx.enter_context(tc.psum_pool(name="psum_out", bufs=4))
+
+        x_sb = keep.tile([P, GROUPS, FEATURES], BF16)
+        nc.sync.dma_start(
+            out=x_sb[:], in_=x.flatten_outer_dims().rearrange("(p a) d -> p a d", a=GROUPS)
+        )
+        w_sb = keep.tile([P, OUTS // P, K], BF16)
+        nc.sync.dma_start(out=w_sb[:], in_=spline_weight.rearrange("(c q) k -> q c k", q=P))
+
+        knots_bf = keep.tile([P, KNOTS], BF16)
+        gain_bf = keep.tile([P, 1], BF16)
+        shift_bf = keep.tile([P, 1], BF16)
+        with nc.allow_non_contiguous_dma(reason="one gain and one shift for each partition"):
+            for h in range(2):
+                rows = slice(h, P, 2)
+                nc.scalar.dma_start(
+                    out=knots_bf[rows, :],
+                    in_=grid_bs[PACK * h : PACK * h + KNOTS].partition_broadcast(FEATURES),
+                )
+                nc.scalar.dma_start(out=gain_bf[rows, :], in_=ln_w.rearrange("(d o) -> d o", o=1))
+                nc.scalar.dma_start(out=shift_bf[rows, :], in_=ln_b.rearrange("(d o) -> d o", o=1))
+
+        one = keep.tile([P, 1], F32)
+        nc.vector.memset(one[:], 1.0)
+        warm = keep.tile([P, 1], F32)
+        nc.scalar.activation(out=warm[:], in_=one[:], func=ACT.Sqrt)
+
+        ident = keep.tile([P, P], F32)
+        make_identity(nc, ident[:])
+
+        stats = keep.tile([P, GROUPS, 6], F32)
+        mean_var = keep.tile([P, GROUPS, 2], F32)
+        for a in range(GROUPS):
+            nc.vector.bn_stats(out=stats[:, a, :], in_=x_sb[:, a, :])
+        for a in range(GROUPS):
+            nc.vector.bn_aggr(out=mean_var[:, a, :], in_=stats[:, a, :])
+        var_eps = keep.tile([P, GROUPS], F32)
+        nc.vector.tensor_scalar(
+            out=var_eps[:], in0=mean_var[:, :, 1], scalar1=EPS, scalar2=None, op0=ALU.add
+        )
+        std = keep.tile([P, GROUPS], F32)
+        nc.scalar.activation(out=std[:], in_=var_eps[:], func=ACT.Sqrt)
+        rstd = keep.tile([P, GROUPS], F32)
+        nc.vector.reciprocal(out=rstd[:], in_=std[:])
+        z_twice = keep.tile([P, GROUPS, FEATURES, 2], F32)
+        for a in range(GROUPS):
+            nc.vector.tensor_scalar(
+                out=z_twice[:, a, :, :],
+                in0=x_sb[:, a, :].unsqueeze(2).to_broadcast([P, FEATURES, 2]),
+                scalar1=mean_var[:, a, 0:1],
+                scalar2=rstd[:, a : a + 1],
+                op0=ALU.subtract,
+                op1=ALU.mult,
+            )
+
+        knots = keep.tile([P, KNOTS], F32)
+        nc.vector.tensor_copy(out=knots[:], in_=knots_bf[:])
+        gain = keep.tile([P, 1], F32)
+        nc.vector.tensor_copy(out=gain[:], in_=gain_bf[:])
+        shift = keep.tile([P, 1], F32)
+        nc.vector.tensor_copy(out=shift[:], in_=shift_bf[:])
+        span = {}
+        for n in range(1, 5):
+            span[n] = keep.tile([P, KNOTS - n], F32, name="span%d" % n)
+            nc.vector.tensor_sub(out=span[n][:], in0=knots[:, n:KNOTS], in1=knots[:, 0 : KNOTS - n])
+        rise_amp = keep.tile([P, CUBES], F32)
+        nc.vector.tensor_mul(out=rise_amp[:], in0=span[1][:, 0:CUBES], in1=span[2][:, 0:CUBES])
+        nc.vector.tensor_mul(out=rise_amp[:], in0=rise_amp[:], in1=span[3][:, 0:CUBES])
+        nc.vector.reciprocal(out=rise_amp[:], in_=rise_amp[:])
+        fall_amp = keep.tile([P, CUBES], F32)
+        nc.vector.tensor_mul(
+            out=fall_amp[:], in0=span[1][:, 2 : 2 + CUBES], in1=span[2][:, 1 : 1 + CUBES]
+        )
+        nc.vector.tensor_mul(out=fall_amp[:], in0=fall_amp[:], in1=span[3][:, 0:CUBES])
+        nc.vector.reciprocal(out=fall_amp[:], in_=fall_amp[:])
+        inv_span1 = keep.tile([P, KNOTS - 1], F32)
+        nc.vector.reciprocal(out=inv_span1[:], in_=span[1][:])
+        left_mix = keep.tile([P, PACK], F32)
+        nc.vector.scalar_tensor_tensor(
+            out=left_mix[:], in0=span[4][:], scalar=-1.0, in1=inv_span1[:, 0:PACK],
+            op0=ALU.mult, op1=ALU.mult,
+        )
+        right_mix = keep.tile([P, PACK], F32)
+        nc.vector.scalar_tensor_tensor(
+            out=right_mix[:], in0=span[4][:], scalar=-1.0, in1=inv_span1[:, 3 : 3 + PACK],
+            op0=ALU.mult, op1=ALU.mult,
+        )
+        offset = keep.tile([P, KNOTS], F32)
+        nc.vector.tensor_scalar(
+            out=offset[:], in0=knots[:], scalar1=-1.0, scalar2=shift[:, 0:1],
+            op0=ALU.mult, op1=ALU.add,
+        )
+        rise_scale = keep.tile([P, CUBES], F32)
+        nc.vector.tensor_scalar(
+            out=rise_scale[:], in0=rise_amp[:], scalar1=gain[:, 0:1], scalar2=None, op0=ALU.mult
+        )
+        rise_bias = keep.tile([P, CUBES], F32)
+        nc.vector.tensor_mul(out=rise_bias[:], in0=rise_amp[:], in1=offset[:, 0:CUBES])
+        fall_scale = keep.tile([P, CUBES], F32)
+        nc.vector.tensor_scalar(
+            out=fall_scale[:], in0=fall_amp[:], scalar1=gain[:, 0:1], scalar2=-1.0,
+            op0=ALU.mult, op1=ALU.mult,
+        )
+        fall_bias = keep.tile([P, CUBES], F32)
+        nc.vector.scalar_tensor_tensor(
+            out=fall_bias[:], in0=fall_amp[:], scalar=-1.0, in1=offset[:, FIRST_FALL:KNOTS],
+            op0=ALU.mult, op1=ALU.mult,
+        )
+
+        w_words = w_sb[:].bitcast(F32)
+        w_grouped = keep.tile([P, OUTS, PACK], BF16, align_bytes=64)
+        w_grouped_words = w_grouped[:].bitcast(F32)
+        for half in range(2):
+            w_t = psum_w.tile([P, 2, 2 * P], F32)
+            for c in range(2):
+                for u in range(2):
+                    nc.tensor.transpose(
+                        w_t[:, u, c * P : (c + 1) * P],
+                        w_words[:, 2 * half + c, u : K // 2 : 2],
+                        ident[:],
+                    )
+            nc.scalar.copy(
+                out=w_grouped_words[:, 2 * P * half : 2 * P * (half + 1), :],
+                in_=w_t[:].rearrange("p u o -> p o u"),
+            )
+        w_codes = keep.tile([P, OUTS], U32, align_bytes=64)
+        w_scales = keep.tile([P, OUTS], U8, align_bytes=64)
+        nc.vector.quantize_mx(
+            out=w_codes[:].bitcast(FP8X4),
+            scales=w_scales[:],
+            in_=w_grouped[:].rearrange("p o t -> p (o t)"),
+        )
+
+        out_rows = out.flatten_outer_dims().rearrange("(p a) o -> p a o", a=GROUPS)
+        out_sb = keep.tile([P, GROUPS, OUTS], F32)
+        for chunk in range(CHUNKS):
+            z_t = psum_z.tile([P, CHUNK], F32)
+            for i in range(CHUNK_GROUPS):
+                nc.tensor.transpose(
+                    z_t[:, i * P : (i + 1) * P],
+                    z_twice[:, chunk * CHUNK_GROUPS + i, :, :].rearrange("p d h -> p (d h)"),
+                    ident[:],
+                )
+
+            square = work.tile([P, KNOTS, CHUNK], F32)
+            rise = work.tile([P, CUBES, CHUNK], F32)
+            fall = work.tile([P, CUBES, CHUNK], F32)
+            left = work.tile([P, PACK, CHUNK], F32)
+            right = work.tile([P, PACK, CHUNK], F32)
+            for j in range(KNOTS):
+                nc.scalar.activation(
+                    out=square[:, j, :], in_=z_t[:], func=ACT.Square,
+                    scale=gain[:, 0:1], bias=offset[:, j : j + 1],
+                )
+                if j < CUBES:
+                    nc.scalar.activation(
+                        out=rise[:, j, :], in_=z_t[:], func=ACT.Relu,
+                        scale=rise_scale[:, j : j + 1], bias=rise_bias[:, j : j + 1],
+                    )
+                    nc.vector.tensor_mul(out=rise[:, j, :], in0=rise[:, j, :], in1=square[:, j, :])
+                if j >= FIRST_FALL:
+                    m = j - FIRST_FALL
+                    nc.scalar.activation(
+                        out=fall[:, m, :], in_=z_t[:], func=ACT.Relu,
+                        scale=fall_scale[:, m : m + 1], bias=fall_bias[:, m : m + 1],
+                    )
+                    nc.vector.tensor_mul(out=fall[:, m, :], in0=fall[:, m, :], in1=square[:, j, :])
+            for g in range(PACK):
+                nc.vector.scalar_tensor_tensor(
+                    out=left[:, g, :], in0=rise[:, g + 1, :], scalar=left_mix[:, g : g + 1],
+                    in1=rise[:, g, :], op0=ALU.mult, op1=ALU.add,
+                )
+                nc.vector.scalar_tensor_tensor(
+                    out=right[:, g, :], in0=fall[:, g, :], scalar=right_mix[:, g : g + 1],
+                    in1=fall[:, g + 1, :], op0=ALU.mult, op1=ALU.add,
+                )
+
+            basis = work.tile([P, CHUNK, PACK], BF16, align_bytes=64)
+            nc.vector.tensor_tensor(
+                out=basis[:],
+                in0=left[:].rearrange("p g n -> p n g"),
+                in1=right[:].rearrange("p g n -> p n g"),
+                op=ALU.max,
+            )
+            codes = work.tile([P, CHUNK], U32, align_bytes=64)
+            scales = work.tile([P, CHUNK], U8, align_bytes=64)
+            nc.vector.quantize_mx(
+                out=codes[:].bitcast(FP8X4),
+                scales=scales[:],
+                in_=basis[:].rearrange("p n g -> p (n g)"),
+            )
+
+            for i in range(CHUNK_GROUPS):
+                a = chunk * CHUNK_GROUPS + i
+                tokens = slice(i * P, (i + 1) * P)
+                acc = psum_out.tile([P, OUTS], F32)
+                nc.tensor.matmul_mx(
+                    out=acc[:],
+                    lhsT=codes[:, tokens].bitcast(FP8X4),
+                    lhsT_scale=scales[:, tokens],
+                    rhs=w_codes[:].bitcast(FP8X4),
+                    rhs_scale=w_scales[:],
+                    start=True,
+                    stop=True,
+                )
+                nc.scalar.copy(out=out_sb[:, a, :], in_=acc[:])
+                nc.sync.dma_start(out=out_rows[:, a, :], in_=out_sb[:, a, :])

@@ -25,7 +25,6 @@ CHUNKS = GROUPS // CHUNK_GROUPS
 CHUNK = CHUNK_GROUPS * P
 KNOTS = PACK + 4
 CUBES = PACK + 1
-FIRST_FALL = KNOTS - CUBES
 
 
 def tile_fc_kanlayer_pb_s_kernel(tc, x, ln_w, ln_b, spline_weight, grid_bs, out):
@@ -65,84 +64,48 @@ def tile_fc_kanlayer_pb_s_kernel(tc, x, ln_w, ln_b, spline_weight, grid_bs, out)
         ident = keep.tile([P, P], F32)
         make_identity(nc, ident[:])
 
-        stats = keep.tile([P, GROUPS, 6], F32)
-        mean_var = keep.tile([P, GROUPS, 2], F32)
-        for a in range(GROUPS):
-            nc.vector.bn_stats(out=stats[:, a, :], in_=x_sb[:, a, :])
-        for a in range(GROUPS):
-            nc.vector.bn_aggr(out=mean_var[:, a, :], in_=stats[:, a, :])
-        var_eps = keep.tile([P, GROUPS], F32)
-        nc.vector.tensor_scalar(
-            out=var_eps[:], in0=mean_var[:, :, 1], scalar1=EPS, scalar2=None, op0=ALU.add
-        )
-        std = keep.tile([P, GROUPS], F32)
-        nc.scalar.activation(out=std[:], in_=var_eps[:], func=ACT.Sqrt)
-        rstd = keep.tile([P, GROUPS], F32)
-        nc.vector.reciprocal(out=rstd[:], in_=std[:])
-        z_twice = keep.tile([P, GROUPS, FEATURES, 2], F32)
-        for a in range(GROUPS):
-            nc.vector.tensor_scalar(
-                out=z_twice[:, a, :, :],
-                in0=x_sb[:, a, :].unsqueeze(2).to_broadcast([P, FEATURES, 2]),
-                scalar1=mean_var[:, a, 0:1],
-                scalar2=rstd[:, a : a + 1],
-                op0=ALU.subtract,
-                op1=ALU.mult,
-            )
-
-        knots = keep.tile([P, KNOTS], F32)
-        nc.vector.tensor_copy(out=knots[:], in_=knots_bf[:])
         gain = keep.tile([P, 1], F32)
         nc.vector.tensor_copy(out=gain[:], in_=gain_bf[:])
-        shift = keep.tile([P, 1], F32)
-        nc.vector.tensor_copy(out=shift[:], in_=shift_bf[:])
-        span = {}
-        for n in range(1, 5):
-            span[n] = keep.tile([P, KNOTS - n], F32, name="span%d" % n)
-            nc.vector.tensor_sub(out=span[n][:], in0=knots[:, n:KNOTS], in1=knots[:, 0 : KNOTS - n])
-        rise_amp = keep.tile([P, CUBES], F32)
-        nc.vector.tensor_mul(out=rise_amp[:], in0=span[1][:, 0:CUBES], in1=span[2][:, 0:CUBES])
-        nc.vector.tensor_mul(out=rise_amp[:], in0=rise_amp[:], in1=span[3][:, 0:CUBES])
-        nc.vector.reciprocal(out=rise_amp[:], in_=rise_amp[:])
-        fall_amp = keep.tile([P, CUBES], F32)
-        nc.vector.tensor_mul(
-            out=fall_amp[:], in0=span[1][:, 2 : 2 + CUBES], in1=span[2][:, 1 : 1 + CUBES]
-        )
-        nc.vector.tensor_mul(out=fall_amp[:], in0=fall_amp[:], in1=span[3][:, 0:CUBES])
-        nc.vector.reciprocal(out=fall_amp[:], in_=fall_amp[:])
-        inv_span1 = keep.tile([P, KNOTS - 1], F32)
-        nc.vector.reciprocal(out=inv_span1[:], in_=span[1][:])
-        left_mix = keep.tile([P, PACK], F32)
-        nc.vector.scalar_tensor_tensor(
-            out=left_mix[:], in0=span[4][:], scalar=-1.0, in1=inv_span1[:, 0:PACK],
-            op0=ALU.mult, op1=ALU.mult,
-        )
-        right_mix = keep.tile([P, PACK], F32)
-        nc.vector.scalar_tensor_tensor(
-            out=right_mix[:], in0=span[4][:], scalar=-1.0, in1=inv_span1[:, 3 : 3 + PACK],
-            op0=ALU.mult, op1=ALU.mult,
-        )
         offset = keep.tile([P, KNOTS], F32)
         nc.vector.tensor_scalar(
-            out=offset[:], in0=knots[:], scalar1=-1.0, scalar2=shift[:, 0:1],
+            out=offset[:], in0=knots_bf[:], scalar1=-1.0, scalar2=shift_bf[:, 0:1],
             op0=ALU.mult, op1=ALU.add,
         )
-        rise_scale = keep.tile([P, CUBES], F32)
+        reach = keep.tile([P, KNOTS], F32)
         nc.vector.tensor_scalar(
-            out=rise_scale[:], in0=rise_amp[:], scalar1=gain[:, 0:1], scalar2=None, op0=ALU.mult
+            out=reach[:], in0=knots_bf[:], scalar1=knots_bf[:, 0:1], scalar2=None, op0=ALU.subtract
         )
-        rise_bias = keep.tile([P, CUBES], F32)
-        nc.vector.tensor_mul(out=rise_bias[:], in0=rise_amp[:], in1=offset[:, 0:CUBES])
-        fall_scale = keep.tile([P, CUBES], F32)
-        nc.vector.tensor_scalar(
-            out=fall_scale[:], in0=fall_amp[:], scalar1=gain[:, 0:1], scalar2=-1.0,
-            op0=ALU.mult, op1=ALU.mult,
-        )
-        fall_bias = keep.tile([P, CUBES], F32)
-        nc.vector.scalar_tensor_tensor(
-            out=fall_bias[:], in0=fall_amp[:], scalar=-1.0, in1=offset[:, FIRST_FALL:KNOTS],
-            op0=ALU.mult, op1=ALU.mult,
-        )
+        RISE = slice(0, CUBES)
+        FALL = slice(CUBES, 2 * CUBES)
+        STEP = slice(2 * CUBES, 2 * CUBES + KNOTS - 1)
+        den = keep.tile([P, 2 * CUBES + KNOTS - 1], F32)
+        inv = keep.tile([P, 2 * CUBES + KNOTS - 1], F32)
+        step = den[:, STEP]
+        nc.gpsimd.tensor_sub(out=step, in0=knots_bf[:, 1:KNOTS], in1=knots_bf[:, 0 : KNOTS - 1])
+        span2 = keep.tile([P, KNOTS - 2], F32)
+        nc.gpsimd.tensor_sub(out=span2[:], in0=knots_bf[:, 2:KNOTS], in1=knots_bf[:, 0 : KNOTS - 2])
+        span3 = keep.tile([P, KNOTS - 3], F32)
+        nc.gpsimd.tensor_sub(out=span3[:], in0=knots_bf[:, 3:KNOTS], in1=knots_bf[:, 0 : KNOTS - 3])
+        back3 = keep.tile([P, KNOTS - 3], F32)
+        nc.gpsimd.tensor_sub(out=back3[:], in0=knots_bf[:, 0 : KNOTS - 3], in1=knots_bf[:, 3:KNOTS])
+        span4 = keep.tile([P, KNOTS - 4], F32)
+        nc.gpsimd.tensor_sub(out=span4[:], in0=knots_bf[:, 4:KNOTS], in1=knots_bf[:, 0 : KNOTS - 4])
+        nc.gpsimd.tensor_mul(out=den[:, RISE], in0=step[:, 0:CUBES], in1=span2[:, 0:CUBES])
+        nc.gpsimd.tensor_mul(out=den[:, RISE], in0=den[:, RISE], in1=span3[:])
+        nc.gpsimd.tensor_mul(out=den[:, FALL], in0=step[:, 2 : 2 + CUBES], in1=span2[:, 1 : 1 + CUBES])
+        nc.gpsimd.tensor_mul(out=den[:, FALL], in0=den[:, FALL], in1=back3[:])
+        nc.vector.reciprocal(out=inv[:], in_=den[:])
+        rise = inv[:, RISE]
+        minus_fall = inv[:, FALL]
+        inv_step = inv[:, STEP]
+        left_lead = rise[:, 0:PACK]
+        right_lead = minus_fall[:, 1:CUBES]
+        left_tail = keep.tile([P, PACK], F32)
+        nc.gpsimd.tensor_mul(out=left_tail[:], in0=span4[:], in1=inv_step[:, 0:PACK])
+        nc.gpsimd.tensor_mul(out=left_tail[:], in0=left_tail[:], in1=rise[:, 1:CUBES])
+        right_tail = keep.tile([P, PACK], F32)
+        nc.gpsimd.tensor_mul(out=right_tail[:], in0=span4[:], in1=inv_step[:, 3 : 3 + PACK])
+        nc.gpsimd.tensor_mul(out=right_tail[:], in0=right_tail[:], in1=minus_fall[:, 0:PACK])
 
         w_words = w_sb[:].bitcast(F32)
         w_grouped = keep.tile([P, OUTS, PACK], BF16, align_bytes=64)
@@ -171,65 +134,90 @@ def tile_fc_kanlayer_pb_s_kernel(tc, x, ln_w, ln_b, spline_weight, grid_bs, out)
         out_rows = out.flatten_outer_dims().rearrange("(p a) o -> p a o", a=GROUPS)
         out_sb = keep.tile([P, GROUPS, OUTS], F32)
         for chunk in range(CHUNKS):
-            z_t = psum_z.tile([P, CHUNK], F32)
+            groups = range(chunk * CHUNK_GROUPS, (chunk + 1) * CHUNK_GROUPS)
+            stats = work.tile([P, CHUNK_GROUPS, 6], F32)
+            mean_var = work.tile([P, CHUNK_GROUPS, 2], F32)
+            for i, a in enumerate(groups):
+                nc.vector.bn_stats(out=stats[:, i, :], in_=x_sb[:, a, :])
             for i in range(CHUNK_GROUPS):
+                nc.vector.bn_aggr(out=mean_var[:, i, :], in_=stats[:, i, :])
+            rstd = work.tile([P, CHUNK_GROUPS], F32)
+            nc.vector.tensor_scalar(
+                out=rstd[:], in0=mean_var[:, :, 1], scalar1=EPS, scalar2=None, op0=ALU.add
+            )
+            nc.scalar.activation(out=rstd[:], in_=rstd[:], func=ACT.Sqrt)
+            nc.vector.reciprocal(out=rstd[:], in_=rstd[:])
+            z_twice = work.tile([P, CHUNK_GROUPS, FEATURES, 2], F32)
+            z_t = psum_z.tile([P, CHUNK], F32)
+            for i, a in enumerate(groups):
+                nc.vector.tensor_scalar(
+                    out=z_twice[:, i, :, :],
+                    in0=x_sb[:, a, :].unsqueeze(2).to_broadcast([P, FEATURES, 2]),
+                    scalar1=mean_var[:, i, 0:1],
+                    scalar2=rstd[:, i : i + 1],
+                    op0=ALU.subtract,
+                    op1=ALU.mult,
+                )
                 nc.tensor.transpose(
                     z_t[:, i * P : (i + 1) * P],
-                    z_twice[:, chunk * CHUNK_GROUPS + i, :, :].rearrange("p d h -> p (d h)"),
+                    z_twice[:, i, :, :].rearrange("p d h -> p (d h)"),
                     ident[:],
                 )
 
-            square = work.tile([P, KNOTS, CHUNK], F32)
-            rise = work.tile([P, CUBES, CHUNK], F32)
-            fall = work.tile([P, CUBES, CHUNK], F32)
-            left = work.tile([P, PACK, CHUNK], F32)
-            right = work.tile([P, PACK, CHUNK], F32)
+            above = work.tile([P, CHUNK], F32)
+            nc.scalar.activation(
+                out=above[:], in_=z_t[:], func=ACT.Identity, scale=gain[:, 0:1], bias=offset[:, 0:1]
+            )
+            cube = work.tile([P, KNOTS, CHUNK], F32)
             for j in range(KNOTS):
                 nc.scalar.activation(
-                    out=square[:, j, :], in_=z_t[:], func=ACT.Square,
+                    out=cube[:, j, :], in_=z_t[:], func=ACT.Square,
                     scale=gain[:, 0:1], bias=offset[:, j : j + 1],
                 )
-                if j < CUBES:
-                    nc.scalar.activation(
-                        out=rise[:, j, :], in_=z_t[:], func=ACT.Relu,
-                        scale=rise_scale[:, j : j + 1], bias=rise_bias[:, j : j + 1],
-                    )
-                    nc.vector.tensor_mul(out=rise[:, j, :], in0=rise[:, j, :], in1=square[:, j, :])
-                if j >= FIRST_FALL:
-                    m = j - FIRST_FALL
-                    nc.scalar.activation(
-                        out=fall[:, m, :], in_=z_t[:], func=ACT.Relu,
-                        scale=fall_scale[:, m : m + 1], bias=fall_bias[:, m : m + 1],
-                    )
-                    nc.vector.tensor_mul(out=fall[:, m, :], in0=fall[:, m, :], in1=square[:, j, :])
+                nc.vector.scalar_tensor_tensor(
+                    out=cube[:, j, :], in0=above[:], scalar=reach[:, j : j + 1], in1=cube[:, j, :],
+                    op0=ALU.subtract, op1=ALU.mult,
+                )
+            left = work.tile([P, PACK, CHUNK], F32)
+            right = work.tile([P, PACK, CHUNK], F32)
+            for g in range(PACK):
+                nc.scalar.activation(
+                    out=left[:, g, :], in_=cube[:, g + 1, :], func=ACT.Relu,
+                    scale=left_tail[:, g : g + 1],
+                )
+                nc.scalar.activation(
+                    out=right[:, g, :], in_=cube[:, g + 3, :], func=ACT.Relu,
+                    scale=right_tail[:, g : g + 1],
+                )
             for g in range(PACK):
                 nc.vector.scalar_tensor_tensor(
-                    out=left[:, g, :], in0=rise[:, g + 1, :], scalar=left_mix[:, g : g + 1],
-                    in1=rise[:, g, :], op0=ALU.mult, op1=ALU.add,
+                    out=left[:, g, :], in0=cube[:, g, :], scalar=left_lead[:, g : g + 1],
+                    in1=left[:, g, :], op0=ALU.mult, op1=ALU.subtract,
                 )
                 nc.vector.scalar_tensor_tensor(
-                    out=right[:, g, :], in0=fall[:, g, :], scalar=right_mix[:, g : g + 1],
-                    in1=fall[:, g + 1, :], op0=ALU.mult, op1=ALU.add,
+                    out=right[:, g, :], in0=cube[:, g + 4, :], scalar=right_lead[:, g : g + 1],
+                    in1=right[:, g, :], op0=ALU.mult, op1=ALU.subtract,
                 )
 
             basis = work.tile([P, CHUNK, PACK], BF16, align_bytes=64)
-            nc.vector.tensor_tensor(
-                out=basis[:],
-                in0=left[:].rearrange("p g n -> p n g"),
-                in1=right[:].rearrange("p g n -> p n g"),
-                op=ALU.max,
-            )
             codes = work.tile([P, CHUNK], U32, align_bytes=64)
             scales = work.tile([P, CHUNK], U8, align_bytes=64)
-            nc.vector.quantize_mx(
-                out=codes[:].bitcast(FP8X4),
-                scales=scales[:],
-                in_=basis[:].rearrange("p n g -> p (n g)"),
-            )
-
             for i in range(CHUNK_GROUPS):
                 a = chunk * CHUNK_GROUPS + i
                 tokens = slice(i * P, (i + 1) * P)
+                nc.vector.scalar_tensor_tensor(
+                    out=basis[:, tokens, :],
+                    in0=left[:, :, tokens].rearrange("p g n -> p n g"),
+                    scalar=0.0,
+                    in1=right[:, :, tokens].rearrange("p g n -> p n g"),
+                    op0=ALU.max,
+                    op1=ALU.max,
+                )
+                nc.vector.quantize_mx(
+                    out=codes[:, tokens].bitcast(FP8X4),
+                    scales=scales[:, tokens],
+                    in_=basis[:, tokens, :].rearrange("p n g -> p (n g)"),
+                )
                 acc = psum_out.tile([P, OUTS], F32)
                 nc.tensor.matmul_mx(
                     out=acc[:],
@@ -240,5 +228,8 @@ def tile_fc_kanlayer_pb_s_kernel(tc, x, ln_w, ln_b, spline_weight, grid_bs, out)
                     start=True,
                     stop=True,
                 )
-                nc.scalar.copy(out=out_sb[:, a, :], in_=acc[:])
+                if chunk == CHUNKS - 1 and i % 2 == 1:
+                    nc.vector.tensor_copy(out=out_sb[:, a, :], in_=acc[:])
+                else:
+                    nc.scalar.copy(out=out_sb[:, a, :], in_=acc[:])
                 nc.sync.dma_start(out=out_rows[:, a, :], in_=out_sb[:, a, :])

@@ -202,17 +202,22 @@ def tile_fc_kanlayer_pb_s_kernel(tc, x, ln_w, ln_b, spline_weight, grid_bs, out)
             basis = work.tile([P, CHUNK, PACK], BF16, align_bytes=64)
             codes = work.tile([P, CHUNK], U32, align_bytes=64)
             scales = work.tile([P, CHUNK], U8, align_bytes=64)
-            for i in range(CHUNK_GROUPS):
+            for step_i in range(CHUNK_GROUPS + 1):
+                if step_i < CHUNK_GROUPS:
+                    tokens = slice(step_i * P, (step_i + 1) * P)
+                    nc.vector.scalar_tensor_tensor(
+                        out=basis[:, tokens, :],
+                        in0=left[:, :, tokens].rearrange("p g n -> p n g"),
+                        scalar=0.0,
+                        in1=right[:, :, tokens].rearrange("p g n -> p n g"),
+                        op0=ALU.max,
+                        op1=ALU.max,
+                    )
+                if step_i == 0:
+                    continue
+                i = step_i - 1
                 a = chunk * CHUNK_GROUPS + i
                 tokens = slice(i * P, (i + 1) * P)
-                nc.vector.scalar_tensor_tensor(
-                    out=basis[:, tokens, :],
-                    in0=left[:, :, tokens].rearrange("p g n -> p n g"),
-                    scalar=0.0,
-                    in1=right[:, :, tokens].rearrange("p g n -> p n g"),
-                    op0=ALU.max,
-                    op1=ALU.max,
-                )
                 nc.vector.quantize_mx(
                     out=codes[:, tokens].bitcast(FP8X4),
                     scales=scales[:, tokens],

@@ -20,9 +20,9 @@ OUTS = 512
 K = 512
 EPS = 1e-5
 GROUPS = 8
-CHUNK_GROUPS = 4
-CHUNKS = GROUPS // CHUNK_GROUPS
-CHUNK = CHUNK_GROUPS * P
+TOKENS = GROUPS * P
+BANK = 512
+BANK_GROUPS = BANK // P
 KNOTS = PACK + 4
 CUBES = PACK + 1
 
@@ -31,7 +31,6 @@ def tile_fc_kanlayer_pb_s_kernel(tc, x, ln_w, ln_b, spline_weight, grid_bs, out)
     nc = tc.nc
     with ExitStack() as ctx:
         keep = ctx.enter_context(tc.tile_pool(name="keep", bufs=1))
-        work = ctx.enter_context(tc.tile_pool(name="work", bufs=2))
         psum_z = ctx.enter_context(tc.psum_pool(name="psum_z", bufs=2))
         psum_w = ctx.enter_context(tc.psum_pool(name="psum_w", bufs=2))
         psum_out = ctx.enter_context(tc.psum_pool(name="psum_out", bufs=4))
@@ -63,6 +62,39 @@ def tile_fc_kanlayer_pb_s_kernel(tc, x, ln_w, ln_b, spline_weight, grid_bs, out)
 
         ident = keep.tile([P, P], F32)
         make_identity(nc, ident[:])
+
+        z_twice = keep.tile([P, GROUPS, FEATURES, 2], F32)
+        z_banks = []
+        for b in range(GROUPS // BANK_GROUPS):
+            groups = range(b * BANK_GROUPS, (b + 1) * BANK_GROUPS)
+            stats = keep.tile([P, BANK_GROUPS, 6], F32, name="stats%d" % b)
+            mean_var = keep.tile([P, BANK_GROUPS, 2], F32, name="mean_var%d" % b)
+            for i, a in enumerate(groups):
+                nc.vector.bn_stats(out=stats[:, i, :], in_=x_sb[:, a, :])
+            for i in range(BANK_GROUPS):
+                nc.vector.bn_aggr(out=mean_var[:, i, :], in_=stats[:, i, :])
+            rstd = keep.tile([P, BANK_GROUPS], F32, name="rstd%d" % b)
+            nc.vector.tensor_scalar(
+                out=rstd[:], in0=mean_var[:, :, 1], scalar1=EPS, scalar2=None, op0=ALU.add
+            )
+            nc.scalar.activation(out=rstd[:], in_=rstd[:], func=ACT.Sqrt)
+            nc.vector.reciprocal(out=rstd[:], in_=rstd[:])
+            z_t = psum_z.tile([P, BANK], F32)
+            for i, a in enumerate(groups):
+                nc.vector.tensor_scalar(
+                    out=z_twice[:, a, :, :],
+                    in0=x_sb[:, a, :].unsqueeze(2).to_broadcast([P, FEATURES, 2]),
+                    scalar1=mean_var[:, i, 0:1],
+                    scalar2=rstd[:, i : i + 1],
+                    op0=ALU.subtract,
+                    op1=ALU.mult,
+                )
+                nc.tensor.transpose(
+                    z_t[:, i * P : (i + 1) * P],
+                    z_twice[:, a, :, :].rearrange("p d h -> p (d h)"),
+                    ident[:],
+                )
+            z_banks.append(z_t)
 
         gain = keep.tile([P, 1], F32)
         nc.vector.tensor_copy(out=gain[:], in_=gain_bf[:])
@@ -131,110 +163,78 @@ def tile_fc_kanlayer_pb_s_kernel(tc, x, ln_w, ln_b, spline_weight, grid_bs, out)
             in_=w_grouped[:].rearrange("p o t -> p (o t)"),
         )
 
-        out_rows = out.flatten_outer_dims().rearrange("(p a) o -> p a o", a=GROUPS)
-        out_sb = keep.tile([P, GROUPS, OUTS], F32)
-        for chunk in range(CHUNKS):
-            groups = range(chunk * CHUNK_GROUPS, (chunk + 1) * CHUNK_GROUPS)
-            stats = work.tile([P, CHUNK_GROUPS, 6], F32)
-            mean_var = work.tile([P, CHUNK_GROUPS, 2], F32)
-            for i, a in enumerate(groups):
-                nc.vector.bn_stats(out=stats[:, i, :], in_=x_sb[:, a, :])
-            for i in range(CHUNK_GROUPS):
-                nc.vector.bn_aggr(out=mean_var[:, i, :], in_=stats[:, i, :])
-            rstd = work.tile([P, CHUNK_GROUPS], F32)
-            nc.vector.tensor_scalar(
-                out=rstd[:], in0=mean_var[:, :, 1], scalar1=EPS, scalar2=None, op0=ALU.add
-            )
-            nc.scalar.activation(out=rstd[:], in_=rstd[:], func=ACT.Sqrt)
-            nc.vector.reciprocal(out=rstd[:], in_=rstd[:])
-            z_twice = work.tile([P, CHUNK_GROUPS, FEATURES, 2], F32)
-            z_t = psum_z.tile([P, CHUNK], F32)
-            for i, a in enumerate(groups):
-                nc.vector.tensor_scalar(
-                    out=z_twice[:, i, :, :],
-                    in0=x_sb[:, a, :].unsqueeze(2).to_broadcast([P, FEATURES, 2]),
-                    scalar1=mean_var[:, i, 0:1],
-                    scalar2=rstd[:, i : i + 1],
-                    op0=ALU.subtract,
-                    op1=ALU.mult,
-                )
-                nc.tensor.transpose(
-                    z_t[:, i * P : (i + 1) * P],
-                    z_twice[:, i, :, :].rearrange("p d h -> p (d h)"),
-                    ident[:],
-                )
-
-            above = work.tile([P, CHUNK], F32)
+        above = keep.tile([P, TOKENS], F32)
+        cube = keep.tile([P, KNOTS, TOKENS], F32)
+        for b, z_t in enumerate(z_banks):
             nc.scalar.activation(
-                out=above[:], in_=z_t[:], func=ACT.Identity, scale=gain[:, 0:1], bias=offset[:, 0:1]
+                out=above[:, b * BANK : (b + 1) * BANK], in_=z_t[:], func=ACT.Identity,
+                scale=gain[:, 0:1], bias=offset[:, 0:1],
             )
-            cube = work.tile([P, KNOTS, CHUNK], F32)
-            for j in range(KNOTS):
+        for j in range(KNOTS):
+            for b, z_t in enumerate(z_banks):
                 nc.scalar.activation(
-                    out=cube[:, j, :], in_=z_t[:], func=ACT.Square,
+                    out=cube[:, j, b * BANK : (b + 1) * BANK], in_=z_t[:], func=ACT.Square,
                     scale=gain[:, 0:1], bias=offset[:, j : j + 1],
                 )
-                nc.vector.scalar_tensor_tensor(
-                    out=cube[:, j, :], in0=above[:], scalar=reach[:, j : j + 1], in1=cube[:, j, :],
-                    op0=ALU.subtract, op1=ALU.mult,
-                )
-            left = work.tile([P, PACK, CHUNK], F32)
-            right = work.tile([P, PACK, CHUNK], F32)
-            for g in range(PACK):
-                nc.scalar.activation(
-                    out=left[:, g, :], in_=cube[:, g + 1, :], func=ACT.Relu,
-                    scale=left_tail[:, g : g + 1],
-                )
-                nc.scalar.activation(
-                    out=right[:, g, :], in_=cube[:, g + 3, :], func=ACT.Relu,
-                    scale=right_tail[:, g : g + 1],
-                )
-            for g in range(PACK):
-                nc.vector.scalar_tensor_tensor(
-                    out=left[:, g, :], in0=cube[:, g, :], scalar=left_lead[:, g : g + 1],
-                    in1=left[:, g, :], op0=ALU.mult, op1=ALU.subtract,
-                )
-                nc.vector.scalar_tensor_tensor(
-                    out=right[:, g, :], in0=cube[:, g + 4, :], scalar=right_lead[:, g : g + 1],
-                    in1=right[:, g, :], op0=ALU.mult, op1=ALU.subtract,
-                )
+            nc.vector.scalar_tensor_tensor(
+                out=cube[:, j, :], in0=above[:], scalar=reach[:, j : j + 1], in1=cube[:, j, :],
+                op0=ALU.subtract, op1=ALU.mult,
+            )
+        left = keep.tile([P, PACK, TOKENS], F32)
+        right = keep.tile([P, PACK, TOKENS], F32)
+        for g in range(PACK):
+            nc.scalar.activation(
+                out=left[:, g, :], in_=cube[:, g + 1, :], func=ACT.Relu,
+                scale=left_tail[:, g : g + 1],
+            )
+            nc.vector.scalar_tensor_tensor(
+                out=left[:, g, :], in0=cube[:, g, :], scalar=left_lead[:, g : g + 1],
+                in1=left[:, g, :], op0=ALU.mult, op1=ALU.subtract,
+            )
+        for g in range(PACK):
+            nc.scalar.activation(
+                out=right[:, g, :], in_=cube[:, g + 3, :], func=ACT.Relu,
+                scale=right_tail[:, g : g + 1],
+            )
+            nc.vector.scalar_tensor_tensor(
+                out=right[:, g, :], in0=cube[:, g + 4, :], scalar=right_lead[:, g : g + 1],
+                in1=right[:, g, :], op0=ALU.mult, op1=ALU.subtract,
+            )
 
-            basis = work.tile([P, CHUNK, PACK], BF16, align_bytes=64)
-            codes = work.tile([P, CHUNK], U32, align_bytes=64)
-            scales = work.tile([P, CHUNK], U8, align_bytes=64)
-            for step_i in range(CHUNK_GROUPS + 1):
-                if step_i < CHUNK_GROUPS:
-                    tokens = slice(step_i * P, (step_i + 1) * P)
-                    nc.vector.scalar_tensor_tensor(
-                        out=basis[:, tokens, :],
-                        in0=left[:, :, tokens].rearrange("p g n -> p n g"),
-                        scalar=0.0,
-                        in1=right[:, :, tokens].rearrange("p g n -> p n g"),
-                        op0=ALU.max,
-                        op1=ALU.max,
-                    )
-                if step_i == 0:
-                    continue
-                i = step_i - 1
-                a = chunk * CHUNK_GROUPS + i
-                tokens = slice(i * P, (i + 1) * P)
-                nc.vector.quantize_mx(
-                    out=codes[:, tokens].bitcast(FP8X4),
-                    scales=scales[:, tokens],
-                    in_=basis[:, tokens, :].rearrange("p n g -> p (n g)"),
+        basis = keep.tile([P, TOKENS, PACK], BF16, align_bytes=64)
+        codes = keep.tile([P, TOKENS], U32, align_bytes=64)
+        scales = keep.tile([P, TOKENS], U8, align_bytes=64)
+        out_sb = keep.tile([P, GROUPS, OUTS], F32)
+        out_rows = out.flatten_outer_dims().rearrange("(p a) o -> p a o", a=GROUPS)
+        for a_max in range(GROUPS + 1):
+            if a_max < GROUPS:
+                tokens = slice(a_max * P, (a_max + 1) * P)
+                nc.vector.scalar_tensor_tensor(
+                    out=basis[:, tokens, :],
+                    in0=left[:, :, tokens].rearrange("p g n -> p n g"),
+                    scalar=0.0,
+                    in1=right[:, :, tokens].rearrange("p g n -> p n g"),
+                    op0=ALU.max,
+                    op1=ALU.max,
                 )
-                acc = psum_out.tile([P, OUTS], F32)
-                nc.tensor.matmul_mx(
-                    out=acc[:],
-                    lhsT=codes[:, tokens].bitcast(FP8X4),
-                    lhsT_scale=scales[:, tokens],
-                    rhs=w_codes[:].bitcast(FP8X4),
-                    rhs_scale=w_scales[:],
-                    start=True,
-                    stop=True,
-                )
-                if chunk == CHUNKS - 1 and i % 2 == 1:
-                    nc.vector.tensor_copy(out=out_sb[:, a, :], in_=acc[:])
-                else:
-                    nc.scalar.copy(out=out_sb[:, a, :], in_=acc[:])
-                nc.sync.dma_start(out=out_rows[:, a, :], in_=out_sb[:, a, :])
+            if a_max == 0:
+                continue
+            a = a_max - 1
+            tokens = slice(a * P, (a + 1) * P)
+            nc.vector.quantize_mx(
+                out=codes[:, tokens].bitcast(FP8X4),
+                scales=scales[:, tokens],
+                in_=basis[:, tokens, :].rearrange("p n g -> p (n g)"),
+            )
+            acc = psum_out.tile([P, OUTS], F32)
+            nc.tensor.matmul_mx(
+                out=acc[:],
+                lhsT=codes[:, tokens].bitcast(FP8X4),
+                lhsT_scale=scales[:, tokens],
+                rhs=w_codes[:].bitcast(FP8X4),
+                rhs_scale=w_scales[:],
+                start=True,
+                stop=True,
+            )
+            nc.scalar.copy(out=out_sb[:, a, :], in_=acc[:])
+            nc.sync.dma_start(out=out_rows[:, a, :], in_=out_sb[:, a, :])

@@ -142,6 +142,7 @@ def tile_fc_kanlayer_pb_s_kernel(tc, x, ln_w, ln_b, spline_weight, grid_bs, out)
         w_words = w_sb[:].bitcast(F32)
         w_grouped = keep.tile([P, OUTS, PACK], BF16, align_bytes=64)
         w_grouped_words = w_grouped[:].bitcast(F32)
+        w_halves = []
         for half in range(2):
             w_t = psum_w.tile([P, 2, 2 * P], F32)
             for c in range(2):
@@ -151,17 +152,9 @@ def tile_fc_kanlayer_pb_s_kernel(tc, x, ln_w, ln_b, spline_weight, grid_bs, out)
                         w_words[:, 2 * half + c, u : K // 2 : 2],
                         ident[:],
                     )
-            nc.scalar.copy(
-                out=w_grouped_words[:, 2 * P * half : 2 * P * (half + 1), :],
-                in_=w_t[:].rearrange("p u o -> p o u"),
-            )
+            w_halves.append(w_t)
         w_codes = keep.tile([P, OUTS], U32, align_bytes=64)
         w_scales = keep.tile([P, OUTS], U8, align_bytes=64)
-        nc.vector.quantize_mx(
-            out=w_codes[:].bitcast(FP8X4),
-            scales=w_scales[:],
-            in_=w_grouped[:].rearrange("p o t -> p (o t)"),
-        )
 
         above = keep.tile([P, TOKENS], F32)
         cube = keep.tile([P, KNOTS, TOKENS], F32)
@@ -206,6 +199,11 @@ def tile_fc_kanlayer_pb_s_kernel(tc, x, ln_w, ln_b, spline_weight, grid_bs, out)
         scales = keep.tile([P, TOKENS], U8, align_bytes=64)
         out_sb = keep.tile([P, GROUPS, OUTS], F32)
         out_rows = out.flatten_outer_dims().rearrange("(p a) o -> p a o", a=GROUPS)
+        for half, w_t in enumerate(w_halves):
+            nc.scalar.copy(
+                out=w_grouped_words[:, 2 * P * half : 2 * P * (half + 1), :],
+                in_=w_t[:].rearrange("p u o -> p o u"),
+            )
         for a_max in range(GROUPS + 1):
             if a_max < GROUPS:
                 tokens = slice(a_max * P, (a_max + 1) * P)
@@ -219,6 +217,12 @@ def tile_fc_kanlayer_pb_s_kernel(tc, x, ln_w, ln_b, spline_weight, grid_bs, out)
                 )
             if a_max == 0:
                 continue
+            if a_max == 1:
+                nc.vector.quantize_mx(
+                    out=w_codes[:].bitcast(FP8X4),
+                    scales=w_scales[:],
+                    in_=w_grouped[:].rearrange("p o t -> p (o t)"),
+                )
             a = a_max - 1
             tokens = slice(a * P, (a + 1) * P)
             nc.vector.quantize_mx(

@@ -74,10 +74,7 @@ def tile_fc_kanlayer_pb_s_kernel(tc, x, ln_w, ln_b, spline_weight, grid_bs, out)
             for i in range(BANK_GROUPS):
                 nc.vector.bn_aggr(out=mean_var[:, i, :], in_=stats[:, i, :])
             rstd = keep.tile([P, BANK_GROUPS], F32, name="rstd%d" % b)
-            nc.vector.tensor_scalar(
-                out=rstd[:], in0=mean_var[:, :, 1], scalar1=EPS, scalar2=None, op0=ALU.add
-            )
-            nc.scalar.activation(out=rstd[:], in_=rstd[:], func=ACT.Sqrt)
+            nc.scalar.activation(out=rstd[:], in_=mean_var[:, :, 1], func=ACT.Sqrt, bias=EPS)
             nc.vector.reciprocal(out=rstd[:], in_=rstd[:])
             z_t = psum_z.tile([P, BANK], F32)
             for i, a in enumerate(groups):
@@ -97,15 +94,14 @@ def tile_fc_kanlayer_pb_s_kernel(tc, x, ln_w, ln_b, spline_weight, grid_bs, out)
             z_banks.append(z_t)
 
         gain = keep.tile([P, 1], F32)
-        nc.vector.tensor_copy(out=gain[:], in_=gain_bf[:])
+        nc.scalar.copy(out=gain[:], in_=gain_bf[:])
         offset = keep.tile([P, KNOTS], F32)
-        nc.vector.tensor_scalar(
-            out=offset[:], in0=knots_bf[:], scalar1=-1.0, scalar2=shift_bf[:, 0:1],
-            op0=ALU.mult, op1=ALU.add,
+        nc.scalar.activation(
+            out=offset[:], in_=knots_bf[:], func=ACT.Identity, scale=-1.0, bias=shift_bf[:, 0:1]
         )
-        reach = keep.tile([P, KNOTS], F32)
-        nc.vector.tensor_scalar(
-            out=reach[:], in0=knots_bf[:], scalar1=knots_bf[:, 0:1], scalar2=None, op0=ALU.subtract
+        minus_reach = keep.tile([P, KNOTS], F32)
+        nc.scalar.activation(
+            out=minus_reach[:], in_=knots_bf[:], func=ACT.Identity, scale=-1.0, bias=knots_bf[:, 0:1]
         )
         RISE = slice(0, CUBES)
         FALL = slice(CUBES, 2 * CUBES)
@@ -116,17 +112,15 @@ def tile_fc_kanlayer_pb_s_kernel(tc, x, ln_w, ln_b, spline_weight, grid_bs, out)
         nc.gpsimd.tensor_sub(out=step, in0=knots_bf[:, 1:KNOTS], in1=knots_bf[:, 0 : KNOTS - 1])
         span2 = keep.tile([P, KNOTS - 2], F32)
         nc.gpsimd.tensor_sub(out=span2[:], in0=knots_bf[:, 2:KNOTS], in1=knots_bf[:, 0 : KNOTS - 2])
-        span3 = keep.tile([P, KNOTS - 3], F32)
-        nc.gpsimd.tensor_sub(out=span3[:], in0=knots_bf[:, 3:KNOTS], in1=knots_bf[:, 0 : KNOTS - 3])
-        back3 = keep.tile([P, KNOTS - 3], F32)
-        nc.gpsimd.tensor_sub(out=back3[:], in0=knots_bf[:, 0 : KNOTS - 3], in1=knots_bf[:, 3:KNOTS])
+        span3 = keep.tile([P, 2 * CUBES], F32)
+        nc.gpsimd.tensor_sub(out=span3[:, RISE], in0=knots_bf[:, 3:KNOTS], in1=knots_bf[:, 0 : KNOTS - 3])
+        nc.gpsimd.tensor_sub(out=span3[:, FALL], in0=knots_bf[:, 0 : KNOTS - 3], in1=knots_bf[:, 3:KNOTS])
+        nc.gpsimd.tensor_mul(out=den[:, RISE], in0=step[:, 0:CUBES], in1=span2[:, 0:CUBES])
+        nc.gpsimd.tensor_mul(out=den[:, FALL], in0=step[:, 2 : 2 + CUBES], in1=span2[:, 1 : 1 + CUBES])
+        nc.gpsimd.tensor_mul(out=den[:, 0 : 2 * CUBES], in0=den[:, 0 : 2 * CUBES], in1=span3[:])
+        nc.vector.reciprocal(out=inv[:], in_=den[:])
         span4 = keep.tile([P, KNOTS - 4], F32)
         nc.gpsimd.tensor_sub(out=span4[:], in0=knots_bf[:, 4:KNOTS], in1=knots_bf[:, 0 : KNOTS - 4])
-        nc.gpsimd.tensor_mul(out=den[:, RISE], in0=step[:, 0:CUBES], in1=span2[:, 0:CUBES])
-        nc.gpsimd.tensor_mul(out=den[:, RISE], in0=den[:, RISE], in1=span3[:])
-        nc.gpsimd.tensor_mul(out=den[:, FALL], in0=step[:, 2 : 2 + CUBES], in1=span2[:, 1 : 1 + CUBES])
-        nc.gpsimd.tensor_mul(out=den[:, FALL], in0=den[:, FALL], in1=back3[:])
-        nc.vector.reciprocal(out=inv[:], in_=den[:])
         rise = inv[:, RISE]
         minus_fall = inv[:, FALL]
         inv_step = inv[:, STEP]
@@ -170,8 +164,8 @@ def tile_fc_kanlayer_pb_s_kernel(tc, x, ln_w, ln_b, spline_weight, grid_bs, out)
                     scale=gain[:, 0:1], bias=offset[:, j : j + 1],
                 )
             nc.vector.scalar_tensor_tensor(
-                out=cube[:, j, :], in0=above[:], scalar=reach[:, j : j + 1], in1=cube[:, j, :],
-                op0=ALU.subtract, op1=ALU.mult,
+                out=cube[:, j, :], in0=above[:], scalar=minus_reach[:, j : j + 1], in1=cube[:, j, :],
+                op0=ALU.add, op1=ALU.mult,
             )
         left = keep.tile([P, PACK, TOKENS], F32)
         right = keep.tile([P, PACK, TOKENS], F32)

@@ -19,6 +19,7 @@ FEATURES = 64
 OUTS = 512
 K = 512
 EPS = 1e-5
+TINY = 2.0 ** -100
 GROUPS = 8
 TOKENS = GROUPS * P
 BANK = 512
@@ -31,8 +32,7 @@ def tile_fc_kanlayer_pb_s_kernel(tc, x, ln_w, ln_b, spline_weight, grid_bs, out)
     nc = tc.nc
     with ExitStack() as ctx:
         keep = ctx.enter_context(tc.tile_pool(name="keep", bufs=1))
-        psum_z = ctx.enter_context(tc.psum_pool(name="psum_z", bufs=2))
-        psum_w = ctx.enter_context(tc.psum_pool(name="psum_w", bufs=2))
+        psum_z = ctx.enter_context(tc.psum_pool(name="psum_z", bufs=4))
         psum_out = ctx.enter_context(tc.psum_pool(name="psum_out", bufs=4))
 
         x_sb = keep.tile([P, GROUPS, FEATURES], BF16)
@@ -76,7 +76,8 @@ def tile_fc_kanlayer_pb_s_kernel(tc, x, ln_w, ln_b, spline_weight, grid_bs, out)
             rstd = keep.tile([P, BANK_GROUPS], F32, name="rstd%d" % b)
             nc.scalar.activation(out=rstd[:], in_=mean_var[:, :, 1], func=ACT.Sqrt, bias=EPS)
             nc.vector.reciprocal(out=rstd[:], in_=rstd[:])
-            z_t = psum_z.tile([P, BANK], F32)
+            z_t = psum_z.tile([P, BANK], F32, name="bank")
+            z_copy = psum_z.tile([P, BANK], F32, name="bank")
             for i, a in enumerate(groups):
                 nc.vector.tensor_scalar(
                     out=z_twice[:, a, :, :],
@@ -91,7 +92,13 @@ def tile_fc_kanlayer_pb_s_kernel(tc, x, ln_w, ln_b, spline_weight, grid_bs, out)
                     z_twice[:, a, :, :].rearrange("p d h -> p (d h)"),
                     ident[:],
                 )
-            z_banks.append(z_t)
+            for i, a in enumerate(groups):
+                nc.tensor.transpose(
+                    z_copy[:, i * P : (i + 1) * P],
+                    z_twice[:, a, :, :].rearrange("p d h -> p (d h)"),
+                    ident[:],
+                )
+            z_banks.append((z_t, z_copy))
 
         gain = keep.tile([P, 1], F32)
         nc.scalar.copy(out=gain[:], in_=gain_bf[:])
@@ -99,9 +106,15 @@ def tile_fc_kanlayer_pb_s_kernel(tc, x, ln_w, ln_b, spline_weight, grid_bs, out)
         nc.scalar.activation(
             out=offset[:], in_=knots_bf[:], func=ACT.Identity, scale=-1.0, bias=shift_bf[:, 0:1]
         )
-        minus_reach = keep.tile([P, KNOTS], F32)
+        divisor = keep.tile([P, 1], F32)
+        nc.scalar.activation(out=divisor[:], in_=gain_bf[:], func=ACT.Abs)
+        nc.scalar.activation(out=divisor[:], in_=divisor[:], func=ACT.Relu, scale=-1.0, bias=TINY)
+        nc.scalar.activation(out=divisor[:], in_=divisor[:], func=ACT.Identity, bias=gain[:, 0:1])
+        inv_divisor = keep.tile([P, 1], F32)
+        nc.vector.reciprocal(out=inv_divisor[:], in_=divisor[:])
+        shift = keep.tile([P, KNOTS], F32)
         nc.scalar.activation(
-            out=minus_reach[:], in_=knots_bf[:], func=ACT.Identity, scale=-1.0, bias=knots_bf[:, 0:1]
+            out=shift[:], in_=offset[:], func=ACT.Identity, scale=inv_divisor[:, 0:1]
         )
         RISE = slice(0, CUBES)
         FALL = slice(CUBES, 2 * CUBES)
@@ -119,6 +132,10 @@ def tile_fc_kanlayer_pb_s_kernel(tc, x, ln_w, ln_b, spline_weight, grid_bs, out)
         nc.gpsimd.tensor_mul(out=den[:, FALL], in0=step[:, 2 : 2 + CUBES], in1=span2[:, 1 : 1 + CUBES])
         nc.gpsimd.tensor_mul(out=den[:, 0 : 2 * CUBES], in0=den[:, 0 : 2 * CUBES], in1=span3[:])
         nc.vector.reciprocal(out=inv[:], in_=den[:])
+        nc.gpsimd.tensor_scalar(
+            out=inv[:, 0 : 2 * CUBES], in0=inv[:, 0 : 2 * CUBES], scalar1=divisor[:, 0:1],
+            scalar2=None, op0=ALU.mult,
+        )
         span4 = keep.tile([P, KNOTS - 4], F32)
         nc.gpsimd.tensor_sub(out=span4[:], in0=knots_bf[:, 4:KNOTS], in1=knots_bf[:, 0 : KNOTS - 4])
         rise = inv[:, RISE]
@@ -133,12 +150,24 @@ def tile_fc_kanlayer_pb_s_kernel(tc, x, ln_w, ln_b, spline_weight, grid_bs, out)
         nc.gpsimd.tensor_mul(out=right_tail[:], in0=span4[:], in1=inv_step[:, 3 : 3 + PACK])
         nc.gpsimd.tensor_mul(out=right_tail[:], in0=right_tail[:], in1=minus_fall[:, 0:PACK])
 
+        cube = keep.tile([P, KNOTS, TOKENS], F32)
+        for j in range(KNOTS):
+            for b, (z_t, z_copy) in enumerate(z_banks):
+                bank = slice(b * BANK, (b + 1) * BANK)
+                nc.scalar.activation(
+                    out=cube[:, j, bank], in_=z_t[:], func=ACT.Square,
+                    scale=gain[:, 0:1], bias=offset[:, j : j + 1],
+                )
+                nc.vector.scalar_tensor_tensor(
+                    out=cube[:, j, bank], in0=z_copy[:], scalar=shift[:, j : j + 1],
+                    in1=cube[:, j, bank], op0=ALU.add, op1=ALU.mult,
+                )
         w_words = w_sb[:].bitcast(F32)
         w_grouped = keep.tile([P, OUTS, PACK], BF16, align_bytes=64)
         w_grouped_words = w_grouped[:].bitcast(F32)
         w_halves = []
         for half in range(2):
-            w_t = psum_w.tile([P, 2, 2 * P], F32)
+            w_t = psum_z.tile([P, 2, 2 * P], F32, name="bank")
             for c in range(2):
                 for u in range(2):
                     nc.tensor.transpose(
@@ -150,23 +179,6 @@ def tile_fc_kanlayer_pb_s_kernel(tc, x, ln_w, ln_b, spline_weight, grid_bs, out)
         w_codes = keep.tile([P, OUTS], U32, align_bytes=64)
         w_scales = keep.tile([P, OUTS], U8, align_bytes=64)
 
-        above = keep.tile([P, TOKENS], F32)
-        cube = keep.tile([P, KNOTS, TOKENS], F32)
-        for b, z_t in enumerate(z_banks):
-            nc.scalar.activation(
-                out=above[:, b * BANK : (b + 1) * BANK], in_=z_t[:], func=ACT.Identity,
-                scale=gain[:, 0:1], bias=offset[:, 0:1],
-            )
-        for j in range(KNOTS):
-            for b, z_t in enumerate(z_banks):
-                nc.scalar.activation(
-                    out=cube[:, j, b * BANK : (b + 1) * BANK], in_=z_t[:], func=ACT.Square,
-                    scale=gain[:, 0:1], bias=offset[:, j : j + 1],
-                )
-            nc.vector.scalar_tensor_tensor(
-                out=cube[:, j, :], in0=above[:], scalar=minus_reach[:, j : j + 1], in1=cube[:, j, :],
-                op0=ALU.add, op1=ALU.mult,
-            )
         left = keep.tile([P, PACK, TOKENS], F32)
         right = keep.tile([P, PACK, TOKENS], F32)
         for g in range(PACK):

@@ -19,21 +19,23 @@ FEATURES = 64
 OUTS = 512
 K = 512
 EPS = 1e-5
-TINY = 2.0 ** -100
 GROUPS = 8
-TOKENS = GROUPS * P
-BANK = 512
-BANK_GROUPS = BANK // P
-KNOTS = PACK + 4
-CUBES = PACK + 1
+HALF = 4
+KNOTS = 12
+FUNCS = 8
+PLAIN = 3
+
+
+def slot(j):
+    return 3 * (j % PACK) + j // PACK
 
 
 def tile_fc_kanlayer_pb_s_kernel(tc, x, ln_w, ln_b, spline_weight, grid_bs, out):
     nc = tc.nc
     with ExitStack() as ctx:
         keep = ctx.enter_context(tc.tile_pool(name="keep", bufs=1))
-        psum_z = ctx.enter_context(tc.psum_pool(name="psum_z", bufs=4))
-        psum_out = ctx.enter_context(tc.psum_pool(name="psum_out", bufs=4))
+        psum = ctx.enter_context(tc.psum_pool(name="psum", bufs=4))
+        psum_right = ctx.enter_context(tc.psum_pool(name="psum_right", bufs=4))
 
         x_sb = keep.tile([P, GROUPS, FEATURES], BF16)
         nc.sync.dma_start(
@@ -41,19 +43,12 @@ def tile_fc_kanlayer_pb_s_kernel(tc, x, ln_w, ln_b, spline_weight, grid_bs, out)
         )
         w_sb = keep.tile([P, OUTS // P, K], BF16)
         nc.sync.dma_start(out=w_sb[:], in_=spline_weight.rearrange("(c q) k -> q c k", q=P))
-
-        knots_bf = keep.tile([P, KNOTS], BF16)
-        gain_bf = keep.tile([P, 1], BF16)
-        shift_bf = keep.tile([P, 1], BF16)
-        with nc.allow_non_contiguous_dma(reason="one gain and one shift for each partition"):
-            for h in range(2):
-                rows = slice(h, P, 2)
-                nc.scalar.dma_start(
-                    out=knots_bf[rows, :],
-                    in_=grid_bs[PACK * h : PACK * h + KNOTS].partition_broadcast(FEATURES),
-                )
-                nc.scalar.dma_start(out=gain_bf[rows, :], in_=ln_w.rearrange("(d o) -> d o", o=1))
-                nc.scalar.dma_start(out=shift_bf[rows, :], in_=ln_b.rearrange("(d o) -> d o", o=1))
+        knots = keep.tile([P, KNOTS], BF16)
+        nc.scalar.dma_start(out=knots[:], in_=grid_bs.partition_broadcast(P))
+        gain_row = keep.tile([P, FEATURES], BF16)
+        nc.scalar.dma_start(out=gain_row[:], in_=ln_w.partition_broadcast(P))
+        shift_row = keep.tile([P, FEATURES], BF16)
+        nc.scalar.dma_start(out=shift_row[:], in_=ln_b.partition_broadcast(P))
 
         one = keep.tile([P, 1], F32)
         nc.vector.memset(one[:], 1.0)
@@ -63,180 +58,242 @@ def tile_fc_kanlayer_pb_s_kernel(tc, x, ln_w, ln_b, spline_weight, grid_bs, out)
         ident = keep.tile([P, P], F32)
         make_identity(nc, ident[:])
 
-        z_twice = keep.tile([P, GROUPS, FEATURES, 2], F32)
-        z_banks = []
-        for b in range(GROUPS // BANK_GROUPS):
-            groups = range(b * BANK_GROUPS, (b + 1) * BANK_GROUPS)
-            stats = keep.tile([P, BANK_GROUPS, 6], F32, name="stats%d" % b)
-            mean_var = keep.tile([P, BANK_GROUPS, 2], F32, name="mean_var%d" % b)
-            for i, a in enumerate(groups):
-                nc.vector.bn_stats(out=stats[:, i, :], in_=x_sb[:, a, :])
-            for i in range(BANK_GROUPS):
-                nc.vector.bn_aggr(out=mean_var[:, i, :], in_=stats[:, i, :])
-            rstd = keep.tile([P, BANK_GROUPS], F32, name="rstd%d" % b)
-            nc.scalar.activation(out=rstd[:], in_=mean_var[:, :, 1], func=ACT.Sqrt, bias=EPS)
-            nc.vector.reciprocal(out=rstd[:], in_=rstd[:])
-            z_t = psum_z.tile([P, BANK], F32, name="bank")
-            z_copy = psum_z.tile([P, BANK], F32, name="bank")
-            for i, a in enumerate(groups):
+        den = keep.tile([P, 29], F32)
+        inv = keep.tile([P, 29], F32)
+        fall_den = keep.tile([P, 9], F32)
+        step = den[:, 18:29]
+        span2 = keep.tile([P, 10], F32)
+        span3 = keep.tile([P, 9], F32)
+        minus_span4 = keep.tile([P, 8], F32)
+        part = keep.tile([P, 2, 9], F32)
+        nc.gpsimd.tensor_sub(out=step, in0=knots[:, 1:12], in1=knots[:, 0:11])
+        nc.gpsimd.tensor_sub(out=span2[:], in0=knots[:, 2:12], in1=knots[:, 0:10])
+        nc.gpsimd.tensor_sub(out=span3[:], in0=knots[:, 3:12], in1=knots[:, 0:9])
+        nc.gpsimd.tensor_mul(out=part[:, 1, :], in0=step[:, 2:11], in1=span2[:, 1:10])
+        nc.gpsimd.tensor_mul(out=fall_den[:], in0=part[:, 1, :], in1=span3[:])
+        nc.gpsimd.tensor_mul(out=part[:, 0, :], in0=step[:, 0:9], in1=span2[:, 0:9])
+        nc.gpsimd.tensor_mul(out=den[:, 0:9], in0=part[:, 0, :], in1=span3[:])
+        nc.gpsimd.tensor_sub(out=minus_span4[:], in0=knots[:, 0:8], in1=knots[:, 4:12])
+
+        ctx.enter_context(
+            tc.manual_schedule(
+                engines={mybir.EngineType.Activation, mybir.EngineType.PE, mybir.EngineType.DVE}
+            )
+        )
+
+        gain = keep.tile([P, FEATURES], F32)
+        shift = keep.tile([P, FEATURES], F32)
+        for src, dst in ((gain_row, gain), (shift_row, shift)):
+            nc.scalar.copy(
+                out=dst[:].rearrange("p (x m) -> p x m", m=4),
+                in_=src[:].rearrange("p (m x) -> p x m", m=4),
+            )
+
+        ctx.enter_context(
+            tc.manual_schedule(
+                engines={mybir.EngineType.Activation, mybir.EngineType.PE, mybir.EngineType.DVE}
+            )
+        )
+
+        halves = range(2)
+        stats = [keep.tile([P, HALF, 6], F32, name="stats%d" % b) for b in halves]
+        mean_var = [keep.tile([P, HALF, 2], F32, name="mean_var%d" % b) for b in halves]
+        rstd = [keep.tile([P, HALF], F32, name="rstd%d" % b) for b in halves]
+        z = [keep.tile([P, HALF, FEATURES], F32, name="z%d" % b) for b in halves]
+        minus_v = keep.tile([P, GROUPS, FEATURES], F32)
+        for b in halves:
+            for i in range(HALF):
+                nc.vector.bn_stats(out=stats[b][:, i, :], in_=x_sb[:, HALF * b + i, :])
+        for b in halves:
+            for i in range(HALF):
+                nc.vector.bn_aggr(out=mean_var[b][:, i, :], in_=stats[b][:, i, :])
+            nc.scalar.activation(out=rstd[b][:], in_=mean_var[b][:, :, 1], func=ACT.Sqrt, bias=EPS)
+        nc.scalar.activation(out=den[:, 9:18], in_=fall_den[:], func=ACT.Sqrt)
+        for b in halves:
+            nc.vector.reciprocal(out=rstd[b][:], in_=rstd[b][:])
+        for b in halves:
+            for i in range(HALF):
                 nc.vector.tensor_scalar(
-                    out=z_twice[:, a, :, :],
-                    in0=x_sb[:, a, :].unsqueeze(2).to_broadcast([P, FEATURES, 2]),
-                    scalar1=mean_var[:, i, 0:1],
-                    scalar2=rstd[:, i : i + 1],
+                    out=z[b][:, i, :].rearrange("p (x m) -> p x m", m=4),
+                    in0=x_sb[:, HALF * b + i, :].rearrange("p (m x) -> p x m", m=4),
+                    scalar1=mean_var[b][:, i, 0:1],
+                    scalar2=rstd[b][:, i : i + 1],
                     op0=ALU.subtract,
                     op1=ALU.mult,
                 )
-                nc.tensor.transpose(
-                    z_t[:, i * P : (i + 1) * P],
-                    z_twice[:, a, :, :].rearrange("p d h -> p (d h)"),
-                    ident[:],
-                )
-            for i, a in enumerate(groups):
-                nc.tensor.transpose(
-                    z_copy[:, i * P : (i + 1) * P],
-                    z_twice[:, a, :, :].rearrange("p d h -> p (d h)"),
-                    ident[:],
-                )
-            z_banks.append((z_t, z_copy))
 
-        gain = keep.tile([P, 1], F32)
-        nc.scalar.copy(out=gain[:], in_=gain_bf[:])
-        offset = keep.tile([P, KNOTS], F32)
-        nc.scalar.activation(
-            out=offset[:], in_=knots_bf[:], func=ACT.Identity, scale=-1.0, bias=shift_bf[:, 0:1]
-        )
-        divisor = keep.tile([P, 1], F32)
-        nc.scalar.activation(out=divisor[:], in_=gain_bf[:], func=ACT.Abs)
-        nc.scalar.activation(out=divisor[:], in_=divisor[:], func=ACT.Relu, scale=-1.0, bias=TINY)
-        nc.scalar.activation(out=divisor[:], in_=divisor[:], func=ACT.Identity, bias=gain[:, 0:1])
-        inv_divisor = keep.tile([P, 1], F32)
-        nc.vector.reciprocal(out=inv_divisor[:], in_=divisor[:])
-        shift = keep.tile([P, KNOTS], F32)
-        nc.scalar.activation(
-            out=shift[:], in_=offset[:], func=ACT.Identity, scale=inv_divisor[:, 0:1]
-        )
-        RISE = slice(0, CUBES)
-        FALL = slice(CUBES, 2 * CUBES)
-        STEP = slice(2 * CUBES, 2 * CUBES + KNOTS - 1)
-        den = keep.tile([P, 2 * CUBES + KNOTS - 1], F32)
-        inv = keep.tile([P, 2 * CUBES + KNOTS - 1], F32)
-        step = den[:, STEP]
-        nc.gpsimd.tensor_sub(out=step, in0=knots_bf[:, 1:KNOTS], in1=knots_bf[:, 0 : KNOTS - 1])
-        span2 = keep.tile([P, KNOTS - 2], F32)
-        nc.gpsimd.tensor_sub(out=span2[:], in0=knots_bf[:, 2:KNOTS], in1=knots_bf[:, 0 : KNOTS - 2])
-        span3 = keep.tile([P, 2 * CUBES], F32)
-        nc.gpsimd.tensor_sub(out=span3[:, RISE], in0=knots_bf[:, 3:KNOTS], in1=knots_bf[:, 0 : KNOTS - 3])
-        nc.gpsimd.tensor_sub(out=span3[:, FALL], in0=knots_bf[:, 0 : KNOTS - 3], in1=knots_bf[:, 3:KNOTS])
-        nc.gpsimd.tensor_mul(out=den[:, RISE], in0=step[:, 0:CUBES], in1=span2[:, 0:CUBES])
-        nc.gpsimd.tensor_mul(out=den[:, FALL], in0=step[:, 2 : 2 + CUBES], in1=span2[:, 1 : 1 + CUBES])
-        nc.gpsimd.tensor_mul(out=den[:, 0 : 2 * CUBES], in0=den[:, 0 : 2 * CUBES], in1=span3[:])
+        def times_gain(b):
+            nc.vector.tensor_mul(
+                out=z[b][:], in0=z[b][:],
+                in1=gain[:].unsqueeze(1).to_broadcast([P, HALF, FEATURES]),
+            )
+
+        def minus_shift(b):
+            nc.vector.scalar_tensor_tensor(
+                out=minus_v[:, HALF * b : HALF * (b + 1), :], in0=z[b][:], scalar=-1.0,
+                in1=shift[:].unsqueeze(1).to_broadcast([P, HALF, FEATURES]),
+                op0=ALU.mult, op1=ALU.subtract,
+            )
+
+        root = inv[:, 9:18]
+        inv_step = inv[:, 18:29]
+        lam = inv[:, 0:9]
+        root_knot = keep.tile([P, 9], F32)
+        minus_beta = keep.tile([P, 8], F32)
+        minus_rho = keep.tile([P, 8], F32)
+        inv_lam = keep.tile([P, 8], F32)
+        minus_lam = keep.tile([P, PACK], F32)
         nc.vector.reciprocal(out=inv[:], in_=den[:])
-        nc.gpsimd.tensor_scalar(
-            out=inv[:, 0 : 2 * CUBES], in0=inv[:, 0 : 2 * CUBES], scalar1=divisor[:, 0:1],
-            scalar2=None, op0=ALU.mult,
-        )
-        span4 = keep.tile([P, KNOTS - 4], F32)
-        nc.gpsimd.tensor_sub(out=span4[:], in0=knots_bf[:, 4:KNOTS], in1=knots_bf[:, 0 : KNOTS - 4])
-        rise = inv[:, RISE]
-        minus_fall = inv[:, FALL]
-        inv_step = inv[:, STEP]
-        left_lead = rise[:, 0:PACK]
-        right_lead = minus_fall[:, 1:CUBES]
-        left_tail = keep.tile([P, PACK], F32)
-        nc.gpsimd.tensor_mul(out=left_tail[:], in0=span4[:], in1=inv_step[:, 0:PACK])
-        nc.gpsimd.tensor_mul(out=left_tail[:], in0=left_tail[:], in1=rise[:, 1:CUBES])
-        right_tail = keep.tile([P, PACK], F32)
-        nc.gpsimd.tensor_mul(out=right_tail[:], in0=span4[:], in1=inv_step[:, 3 : 3 + PACK])
-        nc.gpsimd.tensor_mul(out=right_tail[:], in0=right_tail[:], in1=minus_fall[:, 0:PACK])
+        times_gain(0)
+        nc.vector.tensor_mul(out=root_knot[:], in0=knots[:, 3:12], in1=root)
+        nc.vector.tensor_mul(out=minus_beta[:], in0=minus_span4[:], in1=inv_step[:, 3:11])
+        nc.vector.tensor_mul(out=lam[:, 3:9], in0=lam[:, 3:9], in1=fall_den[:, 0:6])
+        minus_shift(0)
+        nc.vector.tensor_mul(out=minus_rho[:], in0=minus_span4[:], in1=inv_step[:, 0:8])
+        nc.vector.reciprocal(out=inv_lam[:], in_=lam[:, 0:8])
+        times_gain(1)
+        nc.vector.tensor_mul(out=inv_lam[:], in0=inv_lam[:], in1=lam[:, 1:9])
+        minus_shift(1)
+        nc.vector.tensor_mul(out=minus_rho[:], in0=minus_rho[:], in1=inv_lam[:])
 
-        cube = keep.tile([P, KNOTS, TOKENS], F32)
-        for j in range(KNOTS):
-            for b, (z_t, z_copy) in enumerate(z_banks):
-                bank = slice(b * BANK, (b + 1) * BANK)
-                nc.scalar.activation(
-                    out=cube[:, j, bank], in_=z_t[:], func=ACT.Square,
-                    scale=gain[:, 0:1], bias=offset[:, j : j + 1],
-                )
-                nc.vector.scalar_tensor_tensor(
-                    out=cube[:, j, bank], in0=z_copy[:], scalar=shift[:, j : j + 1],
-                    in1=cube[:, j, bank], op0=ALU.add, op1=ALU.mult,
-                )
         w_words = w_sb[:].bitcast(F32)
+        w_sorted = keep.tile([P, OUTS // P, 2, 2, FEATURES], F32)
         w_grouped = keep.tile([P, OUTS, PACK], BF16, align_bytes=64)
         w_grouped_words = w_grouped[:].bitcast(F32)
-        w_halves = []
-        for half in range(2):
-            w_t = psum_z.tile([P, 2, 2 * P], F32, name="bank")
+        w_codes = keep.tile([P, OUTS], U32, align_bytes=64)
+        w_scales = keep.tile([P, OUTS], U8, align_bytes=64)
+
+        def sort_weights(n):
+            u, h = divmod(n, 2)
+            nc.vector.tensor_copy(
+                out=w_sorted[:, :, u, h, :].rearrange("p c (x m) -> p c x m", m=4),
+                in_=w_words[:, :, 2 * h + u : K // 2 : 4].rearrange("p c (m x) -> p c x m", m=4),
+            )
+
+        def transpose_weights(half):
+            w_t = psum.tile([P, 2, 2 * P], F32, name="bank")
             for c in range(2):
                 for u in range(2):
                     nc.tensor.transpose(
                         w_t[:, u, c * P : (c + 1) * P],
-                        w_words[:, 2 * half + c, u : K // 2 : 2],
+                        w_sorted[:, 2 * half + c, u, :, :].rearrange("p h q -> p (h q)"),
                         ident[:],
                     )
-            w_halves.append(w_t)
-        w_codes = keep.tile([P, OUTS], U32, align_bytes=64)
-        w_scales = keep.tile([P, OUTS], U8, align_bytes=64)
+            return w_t
 
-        left = keep.tile([P, PACK, TOKENS], F32)
-        right = keep.tile([P, PACK, TOKENS], F32)
-        for g in range(PACK):
-            nc.scalar.activation(
-                out=left[:, g, :], in_=cube[:, g + 1, :], func=ACT.Relu,
-                scale=left_tail[:, g : g + 1],
-            )
-            nc.vector.scalar_tensor_tensor(
-                out=left[:, g, :], in0=cube[:, g, :], scalar=left_lead[:, g : g + 1],
-                in1=left[:, g, :], op0=ALU.mult, op1=ALU.subtract,
-            )
-        for g in range(PACK):
-            nc.scalar.activation(
-                out=right[:, g, :], in_=cube[:, g + 3, :], func=ACT.Relu,
-                scale=right_tail[:, g : g + 1],
-            )
-            nc.vector.scalar_tensor_tensor(
-                out=right[:, g, :], in0=cube[:, g + 4, :], scalar=right_lead[:, g : g + 1],
-                in1=right[:, g, :], op0=ALU.mult, op1=ALU.subtract,
-            )
-
-        basis = keep.tile([P, TOKENS, PACK], BF16, align_bytes=64)
-        codes = keep.tile([P, TOKENS], U32, align_bytes=64)
-        scales = keep.tile([P, TOKENS], U8, align_bytes=64)
-        out_sb = keep.tile([P, GROUPS, OUTS], F32)
-        out_rows = out.flatten_outer_dims().rearrange("(p a) o -> p a o", a=GROUPS)
-        for half, w_t in enumerate(w_halves):
+        def group_weights(half, w_t):
             nc.scalar.copy(
                 out=w_grouped_words[:, 2 * P * half : 2 * P * (half + 1), :],
                 in_=w_t[:].rearrange("p u o -> p o u"),
             )
-        for a_max in range(GROUPS + 1):
-            if a_max < GROUPS:
-                tokens = slice(a_max * P, (a_max + 1) * P)
-                nc.vector.scalar_tensor_tensor(
-                    out=basis[:, tokens, :],
-                    in0=left[:, :, tokens].rearrange("p g n -> p n g"),
-                    scalar=0.0,
-                    in1=right[:, :, tokens].rearrange("p g n -> p n g"),
-                    op0=ALU.max,
-                    op1=ALU.max,
+
+        def quantise_weights():
+            nc.vector.quantize_mx(
+                out=w_codes[:].bitcast(FP8X4),
+                scales=w_scales[:],
+                in_=w_grouped[:].rearrange("p o t -> p (o t)"),
+            )
+
+        basis = keep.tile([P, GROUPS * P, PACK], BF16, align_bytes=64)
+        codes = keep.tile([P, GROUPS * P], U32, align_bytes=64)
+        scales = keep.tile([P, GROUPS * P], U8, align_bytes=64)
+        out_sb = keep.tile([P, GROUPS, OUTS], F32)
+        out_rows = out.flatten_outer_dims().rearrange("(p a) o -> p a o", a=GROUPS)
+
+        def add_transposed(dst, lead, trail):
+            nc.tensor.matmul(dst, lhsT=lead, rhs=ident[:], is_transpose=True, start=True, stop=False)
+            nc.tensor.matmul(dst, lhsT=trail, rhs=ident[:], is_transpose=True, start=False, stop=True)
+
+        order = (0, 1, 4, 5, 2, 6, 3, 7, 8, 9, 10, 11)
+        cube = keep.tile([P, GROUPS, KNOTS, FEATURES], F32)
+        trail_l = keep.tile([P, GROUPS, PACK, 2, FEATURES], F32)
+        trail_r = keep.tile([P, GROUPS, PACK, 2, FEATURES], F32)
+        left = keep.tile([P, PACK, GROUPS * P], BF16)
+        right = {}
+
+        def square(j, groups=slice(0, GROUPS)):
+            at = cube[:, groups, slot(j), :]
+            if j < PLAIN:
+                nc.scalar.activation(
+                    out=at, in_=minus_v[:, groups, :], func=ACT.Square, bias=knots[:, j : j + 1]
                 )
-            if a_max == 0:
-                continue
-            if a_max == 1:
-                nc.vector.quantize_mx(
-                    out=w_codes[:].bitcast(FP8X4),
-                    scales=w_scales[:],
-                    in_=w_grouped[:].rearrange("p o t -> p (o t)"),
+            else:
+                nc.scalar.activation(
+                    out=at, in_=minus_v[:, groups, :], func=ACT.Square,
+                    scale=root[:, j - 3 : j - 2], bias=root_knot[:, j - 3 : j - 2],
                 )
-            a = a_max - 1
+
+        def make_cube(j, groups=slice(0, GROUPS)):
+            at = cube[:, groups, slot(j), :]
+            nc.vector.scalar_tensor_tensor(
+                out=at, in0=minus_v[:, groups, :], scalar=knots[:, j : j + 1], in1=at,
+                op0=ALU.add, op1=ALU.mult,
+            )
+
+        def make_trails(j):
+            at = cube[:, :, slot(j), :]
+            g = j - 1
+            if 0 <= g < FUNCS:
+                nc.vector.tensor_scalar(
+                    out=trail_l[:, :, g % PACK, g // PACK, :], in0=at,
+                    scalar1=minus_rho[:, g : g + 1], scalar2=0.0, op0=ALU.mult, op1=ALU.max,
+                )
+            g = j - 3
+            if 0 <= g < FUNCS:
+                nc.vector.tensor_scalar(
+                    out=trail_r[:, :, g % PACK, g // PACK, :], in0=at,
+                    scalar1=minus_beta[:, g : g + 1], scalar2=0.0, op0=ALU.mult, op1=ALU.min,
+                )
+
+        def scale_of_left():
+            for h in range(2):
+                rows = slice(64 * h, 64 * h + 64)
+                nc.scalar.activation(
+                    out=minus_lam[rows, :], in_=lam[rows, PACK * h : PACK * h + PACK],
+                    func=ACT.Identity, scale=-1.0,
+                )
+
+        def left_bank(b, t):
+            bank = psum.tile([P, HALF * P], F32, name="bank")
+            for i in range(HALF):
+                add_transposed(
+                    bank[:, i * P : (i + 1) * P],
+                    cube[:, HALF * b + i, slot(t) : slot(t) + 2, :].rearrange("p s q -> p (s q)"),
+                    trail_l[:, HALF * b + i, t, :, :].rearrange("p h q -> p (h q)"),
+                )
+            return bank
+
+        def copy_left(b, t, bank):
+            nc.scalar.activation(
+                out=left[:, t, HALF * P * b : HALF * P * (b + 1)], in_=bank[:], func=ACT.Relu,
+                scale=minus_lam[:, t : t + 1],
+            )
+
+        def right_forms(a, t):
+            if a not in right:
+                right[a] = psum_right.tile([P, PACK, P], F32, name="right")
+            add_transposed(
+                right[a][:, t, :],
+                cube[:, a, slot(t) + 1 : slot(t) + 3, :].rearrange("p s q -> p (s q)"),
+                trail_r[:, a, t, :, :].rearrange("p h q -> p (h q)"),
+            )
+
+        def maximum(a):
+            nc.vector.tensor_tensor(
+                out=basis[:, a * P : (a + 1) * P, :],
+                in0=right[a][:].rearrange("p t n -> p n t"),
+                in1=left[:, :, a * P : (a + 1) * P].rearrange("p t n -> p n t"),
+                op=ALU.max,
+            )
+
+        def product(a):
             tokens = slice(a * P, (a + 1) * P)
             nc.vector.quantize_mx(
                 out=codes[:, tokens].bitcast(FP8X4),
                 scales=scales[:, tokens],
                 in_=basis[:, tokens, :].rearrange("p n g -> p (n g)"),
             )
-            acc = psum_out.tile([P, OUTS], F32)
+            acc = psum.tile([P, OUTS], F32, name="bank")
             nc.tensor.matmul_mx(
                 out=acc[:],
                 lhsT=codes[:, tokens].bitcast(FP8X4),
@@ -246,5 +303,68 @@ def tile_fc_kanlayer_pb_s_kernel(tc, x, ln_w, ln_b, spline_weight, grid_bs, out)
                 start=True,
                 stop=True,
             )
+            return acc
+
+        def store(a, acc):
             nc.scalar.copy(out=out_sb[:, a, :], in_=acc[:])
             nc.sync.dma_start(out=out_rows[:, a, :], in_=out_sb[:, a, :])
+
+        LAST = len(order)
+        left_at = {3: 0, 5: 1, 7: 2, 8: 3}
+        right_at = {8: 0, 9: 1, 10: 2, 11: 3}
+        first, second = slice(0, HALF), slice(HALF, GROUPS)
+        square(order[0], first)
+        square(order[0], second)
+        for n in range(4):
+            sort_weights(n)
+        for k in range(1, 4):
+            square(order[k])
+        scale_of_left()
+        pending = []
+
+        def left_form(b, t):
+            bank = left_bank(b, t)
+            pending.append(lambda: copy_left(b, t, bank))
+
+        second_left_at = {6: 0, 7: 1, 20: 2, 21: 3}
+        for n in range(LAST + 1):
+            if n == 0:
+                make_cube(order[0], first)
+                make_cube(order[0], second)
+            elif n < LAST:
+                make_cube(order[n])
+            if n + 4 < LAST:
+                square(order[n + 4])
+            for f in pending[:1]:
+                f()
+            pending = pending[1:]
+            if n:
+                k = n - 1
+                make_trails(order[k])
+                if k in left_at:
+                    left_form(0, left_at[k])
+                if k in right_at:
+                    for i in range(HALF):
+                        right_forms(i, right_at[k])
+            if n in second_left_at:
+                left_form(1, second_left_at[n])
+            if n in (5, 5+1):
+                w_t = transpose_weights(n - 5)
+                pending.append(lambda half=n - 5, w_t=w_t: group_weights(half, w_t))
+        for f in pending:
+            f()
+        pending = []
+        quantise_weights()
+        for a in range(GROUPS + 1):
+            if a < GROUPS:
+                maximum(a)
+                if a < HALF:
+                    if 20 + a in second_left_at:
+                        left_form(1, second_left_at[20 + a])
+                        for f in pending:
+                            f()
+                        pending = []
+                    for t in range(PACK):
+                        right_forms(a + HALF, t)
+            if a:
+                store(a - 1, product(a - 1))

@@ -66,14 +66,6 @@ def tile_fc_kanlayer_pb_s_kernel(tc, x, ln_w, ln_b, spline_weight, grid_bs, out)
         span3 = keep.tile([P, 9], F32)
         minus_span4 = keep.tile([P, 8], F32)
         part = keep.tile([P, 2, 9], F32)
-        nc.gpsimd.tensor_sub(out=step, in0=knots[:, 1:12], in1=knots[:, 0:11])
-        nc.gpsimd.tensor_sub(out=span2[:], in0=knots[:, 2:12], in1=knots[:, 0:10])
-        nc.gpsimd.tensor_sub(out=span3[:], in0=knots[:, 3:12], in1=knots[:, 0:9])
-        nc.gpsimd.tensor_mul(out=part[:, 1, :], in0=step[:, 2:11], in1=span2[:, 1:10])
-        nc.gpsimd.tensor_mul(out=fall_den[:], in0=part[:, 1, :], in1=span3[:])
-        nc.gpsimd.tensor_mul(out=part[:, 0, :], in0=step[:, 0:9], in1=span2[:, 0:9])
-        nc.gpsimd.tensor_mul(out=den[:, 0:9], in0=part[:, 0, :], in1=span3[:])
-        nc.gpsimd.tensor_sub(out=minus_span4[:], in0=knots[:, 0:8], in1=knots[:, 4:12])
 
         ctx.enter_context(
             tc.manual_schedule(
@@ -108,9 +100,17 @@ def tile_fc_kanlayer_pb_s_kernel(tc, x, ln_w, ln_b, spline_weight, grid_bs, out)
             for i in range(HALF):
                 nc.vector.bn_aggr(out=mean_var[b][:, i, :], in_=stats[b][:, i, :])
             nc.scalar.activation(out=rstd[b][:], in_=mean_var[b][:, :, 1], func=ACT.Sqrt, bias=EPS)
+        nc.vector.tensor_sub(out=step, in0=knots[:, 1:12], in1=knots[:, 0:11])
+        nc.vector.tensor_sub(out=span2[:], in0=knots[:, 2:12], in1=knots[:, 0:10])
+        nc.vector.tensor_sub(out=span3[:], in0=knots[:, 3:12], in1=knots[:, 0:9])
+        nc.vector.tensor_sub(out=minus_span4[:], in0=knots[:, 0:8], in1=knots[:, 4:12])
+        nc.vector.tensor_mul(out=part[:, 1, :], in0=step[:, 2:11], in1=span2[:, 1:10])
+        nc.vector.tensor_mul(out=part[:, 0, :], in0=step[:, 0:9], in1=span2[:, 0:9])
+        nc.vector.reciprocal(out=rstd[0][:], in_=rstd[0][:])
+        nc.vector.tensor_mul(out=fall_den[:], in0=part[:, 1, :], in1=span3[:])
+        nc.vector.reciprocal(out=rstd[1][:], in_=rstd[1][:])
+        nc.vector.tensor_mul(out=den[:, 0:9], in0=part[:, 0, :], in1=span3[:])
         nc.scalar.activation(out=den[:, 9:18], in_=fall_den[:], func=ACT.Sqrt)
-        for b in halves:
-            nc.vector.reciprocal(out=rstd[b][:], in_=rstd[b][:])
         for b in halves:
             for i in range(HALF):
                 nc.vector.tensor_scalar(

@@ -22,6 +22,7 @@ EPS = 1e-5
 GROUPS = 8
 HALF = 4
 KNOTS = 12
+PAD = 16
 FUNCS = 8
 PLAIN = 3
 
@@ -41,19 +42,21 @@ def tile_fc_kanlayer_pb_s_kernel(tc, x, ln_w, ln_b, spline_weight, grid_bs, out)
         nc.sync.dma_start(
             out=x_sb[:], in_=x.flatten_outer_dims().rearrange("(p a) d -> p a d", a=GROUPS)
         )
-        w_sb = keep.tile([P, OUTS // P, K], BF16)
-        nc.sync.dma_start(out=w_sb[:], in_=spline_weight.rearrange("(c q) k -> q c k", q=P))
-        knots = keep.tile([P, KNOTS], BF16)
-        nc.scalar.dma_start(out=knots[:], in_=grid_bs.partition_broadcast(P))
-        gain_row = keep.tile([P, FEATURES], BF16)
-        nc.scalar.dma_start(out=gain_row[:], in_=ln_w.partition_broadcast(P))
-        shift_row = keep.tile([P, FEATURES], BF16)
-        nc.scalar.dma_start(out=shift_row[:], in_=ln_b.partition_broadcast(P))
-
         one = keep.tile([P, 1], F32)
         nc.vector.memset(one[:], 1.0)
         warm = keep.tile([P, 1], F32)
         nc.scalar.activation(out=warm[:], in_=one[:], func=ACT.Sqrt)
+
+        PARAMS = PAD + 2 * FEATURES
+        row = keep.tile([P, PARAMS], BF16)
+        nc.vector.memset(row[:], 0.0)
+        nc.sync.dma_start(out=row[0:1, 0:KNOTS], in_=grid_bs.unsqueeze(0))
+        nc.sync.dma_start(out=row[0:1, PAD : PAD + FEATURES], in_=ln_w.unsqueeze(0))
+        nc.sync.dma_start(out=row[0:1, PAD + FEATURES : PARAMS], in_=ln_b.unsqueeze(0))
+        w_sb = keep.tile([P, OUTS // P, K], BF16)
+        nc.sync.dma_start(out=w_sb[:], in_=spline_weight.rearrange("(c q) k -> q c k", q=P))
+        ones = keep.tile([P, P], BF16)
+        nc.vector.memset(ones[:], 1.0)
 
         ident = keep.tile([P, P], F32)
         make_identity(nc, ident[:])
@@ -73,14 +76,10 @@ def tile_fc_kanlayer_pb_s_kernel(tc, x, ln_w, ln_b, spline_weight, grid_bs, out)
             )
         )
 
-        gain = keep.tile([P, FEATURES], F32)
-        shift = keep.tile([P, FEATURES], F32)
-        for src, dst in ((gain_row, gain), (shift_row, shift)):
-            nc.scalar.copy(
-                out=dst[:].rearrange("p (x m) -> p x m", m=4),
-                in_=src[:].rearrange("p (m x) -> p x m", m=4),
-            )
-
+        params = psum.tile([P, PARAMS], F32, name="bank")
+        nc.tensor.matmul(params[:], lhsT=ones[:], rhs=row[:], start=True, stop=True)
+        knots = keep.tile([P, KNOTS], F32)
+        nc.scalar.copy(out=knots[:], in_=params[:, 0:KNOTS])
         ctx.enter_context(
             tc.manual_schedule(
                 engines={mybir.EngineType.Activation, mybir.EngineType.PE, mybir.EngineType.DVE}
@@ -100,6 +99,16 @@ def tile_fc_kanlayer_pb_s_kernel(tc, x, ln_w, ln_b, spline_weight, grid_bs, out)
             for i in range(HALF):
                 nc.vector.bn_aggr(out=mean_var[b][:, i, :], in_=stats[b][:, i, :])
             nc.scalar.activation(out=rstd[b][:], in_=mean_var[b][:, :, 1], func=ACT.Sqrt, bias=EPS)
+        gain = keep.tile([P, FEATURES], F32)
+        shift = keep.tile([P, FEATURES], F32)
+        for n, dst in ((0, gain), (1, shift)):
+            nc.scalar.copy(
+                out=dst[:].rearrange("p (x m) -> p x m", m=4),
+                in_=params[:, PAD + n * FEATURES : PAD + (n + 1) * FEATURES].rearrange(
+                    "p (m x) -> p x m", m=4
+                ),
+            )
+
         nc.vector.tensor_sub(out=step, in0=knots[:, 1:12], in1=knots[:, 0:11])
         nc.vector.tensor_sub(out=span2[:], in0=knots[:, 2:12], in1=knots[:, 0:10])
         nc.vector.tensor_sub(out=span3[:], in0=knots[:, 3:12], in1=knots[:, 0:9])

@@ -79,92 +79,13 @@ def tile_fc_kanlayer_pb_s_kernel(tc, x, ln_w, ln_b, spline_weight, grid_bs, out)
         params = psum.tile([P, PARAMS], F32, name="bank")
         nc.tensor.matmul(params[:], lhsT=ones[:], rhs=row[:], start=True, stop=True)
         knots = keep.tile([P, KNOTS], F32)
-        nc.scalar.copy(out=knots[:], in_=params[:, 0:KNOTS])
         ctx.enter_context(
             tc.manual_schedule(
                 engines={mybir.EngineType.Activation, mybir.EngineType.PE, mybir.EngineType.DVE}
             )
         )
 
-        halves = range(2)
-        stats = [keep.tile([P, HALF, 6], F32, name="stats%d" % b) for b in halves]
-        mean_var = [keep.tile([P, HALF, 2], F32, name="mean_var%d" % b) for b in halves]
-        rstd = [keep.tile([P, HALF], F32, name="rstd%d" % b) for b in halves]
-        z = [keep.tile([P, HALF, FEATURES], F32, name="z%d" % b) for b in halves]
-        minus_v = keep.tile([P, GROUPS, FEATURES], F32)
-        for b in halves:
-            for i in range(HALF):
-                nc.vector.bn_stats(out=stats[b][:, i, :], in_=x_sb[:, HALF * b + i, :])
-        for b in halves:
-            for i in range(HALF):
-                nc.vector.bn_aggr(out=mean_var[b][:, i, :], in_=stats[b][:, i, :])
-            nc.scalar.activation(out=rstd[b][:], in_=mean_var[b][:, :, 1], func=ACT.Sqrt, bias=EPS)
-        gain = keep.tile([P, FEATURES], F32)
-        shift = keep.tile([P, FEATURES], F32)
-        for n, dst in ((0, gain), (1, shift)):
-            nc.scalar.copy(
-                out=dst[:].rearrange("p (x m) -> p x m", m=4),
-                in_=params[:, PAD + n * FEATURES : PAD + (n + 1) * FEATURES].rearrange(
-                    "p (m x) -> p x m", m=4
-                ),
-            )
-
-        nc.vector.tensor_sub(out=step, in0=knots[:, 1:12], in1=knots[:, 0:11])
-        nc.vector.tensor_sub(out=span2[:], in0=knots[:, 2:12], in1=knots[:, 0:10])
-        nc.vector.tensor_sub(out=span3[:], in0=knots[:, 3:12], in1=knots[:, 0:9])
-        nc.vector.tensor_sub(out=minus_span4[:], in0=knots[:, 0:8], in1=knots[:, 4:12])
-        nc.vector.tensor_mul(out=part[:, 1, :], in0=step[:, 2:11], in1=span2[:, 1:10])
-        nc.vector.tensor_mul(out=part[:, 0, :], in0=step[:, 0:9], in1=span2[:, 0:9])
-        nc.vector.reciprocal(out=rstd[0][:], in_=rstd[0][:])
-        nc.vector.tensor_mul(out=fall_den[:], in0=part[:, 1, :], in1=span3[:])
-        nc.vector.reciprocal(out=rstd[1][:], in_=rstd[1][:])
-        nc.vector.tensor_mul(out=den[:, 0:9], in0=part[:, 0, :], in1=span3[:])
-        nc.scalar.activation(out=den[:, 9:18], in_=fall_den[:], func=ACT.Sqrt)
-        for b in halves:
-            for i in range(HALF):
-                nc.vector.tensor_scalar(
-                    out=z[b][:, i, :].rearrange("p (x m) -> p x m", m=4),
-                    in0=x_sb[:, HALF * b + i, :].rearrange("p (m x) -> p x m", m=4),
-                    scalar1=mean_var[b][:, i, 0:1],
-                    scalar2=rstd[b][:, i : i + 1],
-                    op0=ALU.subtract,
-                    op1=ALU.mult,
-                )
-
-        def times_gain(b):
-            nc.vector.tensor_mul(
-                out=z[b][:], in0=z[b][:],
-                in1=gain[:].unsqueeze(1).to_broadcast([P, HALF, FEATURES]),
-            )
-
-        def minus_shift(b):
-            nc.vector.scalar_tensor_tensor(
-                out=minus_v[:, HALF * b : HALF * (b + 1), :], in0=z[b][:], scalar=-1.0,
-                in1=shift[:].unsqueeze(1).to_broadcast([P, HALF, FEATURES]),
-                op0=ALU.mult, op1=ALU.subtract,
-            )
-
-        root = inv[:, 9:18]
-        inv_step = inv[:, 18:29]
-        lam = inv[:, 0:9]
-        root_knot = keep.tile([P, 9], F32)
-        minus_beta = keep.tile([P, 8], F32)
-        minus_rho = keep.tile([P, 8], F32)
-        inv_lam = keep.tile([P, 8], F32)
-        minus_lam = keep.tile([P, PACK], F32)
-        nc.vector.reciprocal(out=inv[:], in_=den[:])
-        times_gain(0)
-        nc.vector.tensor_mul(out=root_knot[:], in0=knots[:, 3:12], in1=root)
-        nc.vector.tensor_mul(out=minus_beta[:], in0=minus_span4[:], in1=inv_step[:, 3:11])
-        nc.vector.tensor_mul(out=lam[:, 3:9], in0=lam[:, 3:9], in1=fall_den[:, 0:6])
-        minus_shift(0)
-        nc.vector.tensor_mul(out=minus_rho[:], in0=minus_span4[:], in1=inv_step[:, 0:8])
-        nc.vector.reciprocal(out=inv_lam[:], in_=lam[:, 0:8])
-        times_gain(1)
-        nc.vector.tensor_mul(out=inv_lam[:], in0=inv_lam[:], in1=lam[:, 1:9])
-        minus_shift(1)
-        nc.vector.tensor_mul(out=minus_rho[:], in0=minus_rho[:], in1=inv_lam[:])
-
+        VECTOR_SORTS = (0, 1)
         w_words = w_sb[:].bitcast(F32)
         w_sorted = keep.tile([P, OUTS // P, 2, 2, FEATURES], F32)
         w_grouped = keep.tile([P, OUTS, PACK], BF16, align_bytes=64)
@@ -174,7 +95,8 @@ def tile_fc_kanlayer_pb_s_kernel(tc, x, ln_w, ln_b, spline_weight, grid_bs, out)
 
         def sort_weights(n):
             u, h = divmod(n, 2)
-            nc.vector.tensor_copy(
+            copy = nc.vector.tensor_copy if n in VECTOR_SORTS else nc.scalar.copy
+            copy(
                 out=w_sorted[:, :, u, h, :].rearrange("p c (x m) -> p c x m", m=4),
                 in_=w_words[:, :, 2 * h + u : K // 2 : 4].rearrange("p c (m x) -> p c x m", m=4),
             )
@@ -203,6 +125,95 @@ def tile_fc_kanlayer_pb_s_kernel(tc, x, ln_w, ln_b, spline_weight, grid_bs, out)
                 in_=w_grouped[:].rearrange("p o t -> p (o t)"),
             )
 
+        halves = range(2)
+        stats = [keep.tile([P, HALF, 6], F32, name="stats%d" % b) for b in halves]
+        mean_var = [keep.tile([P, HALF, 2], F32, name="mean_var%d" % b) for b in halves]
+        rstd = [keep.tile([P, HALF], F32, name="rstd%d" % b) for b in halves]
+        z = [keep.tile([P, HALF, FEATURES], F32, name="z%d" % b) for b in halves]
+        minus_v = keep.tile([P, GROUPS, FEATURES], F32)
+
+        def statistics(b, i):
+            nc.vector.bn_stats(out=stats[b][:, i, :], in_=x_sb[:, HALF * b + i, :])
+
+        def aggregate(b):
+            for i in range(HALF):
+                nc.vector.bn_aggr(out=mean_var[b][:, i, :], in_=stats[b][:, i, :])
+            nc.scalar.activation(out=rstd[b][:], in_=mean_var[b][:, :, 1], func=ACT.Sqrt, bias=EPS)
+
+        def normalise(b):
+            for i in range(HALF):
+                nc.vector.scalar_tensor_tensor(
+                    out=z[b][:, i, :].rearrange("p (x m) -> p x m", m=4),
+                    in0=x_sb[:, HALF * b + i, :].rearrange("p (m x) -> p x m", m=4),
+                    scalar=mean_var[b][:, i, 0:1],
+                    in1=gain[:].rearrange("p (x m) -> p x m", m=4),
+                    op0=ALU.subtract,
+                    op1=ALU.mult,
+                )
+
+        def apply_shift(b):
+            for i in range(HALF):
+                nc.vector.scalar_tensor_tensor(
+                    out=minus_v[:, HALF * b + i, :], in0=z[b][:, i, :], scalar=rstd[b][:, i : i + 1],
+                    in1=shift[:], op0=ALU.mult, op1=ALU.add,
+                )
+
+        root = inv[:, 9:18]
+        inv_step = inv[:, 18:29]
+        lam = inv[:, 0:9]
+        root_knot = keep.tile([P, 9], F32)
+        minus_beta = keep.tile([P, 8], F32)
+        minus_rho = keep.tile([P, 8], F32)
+        inv_lam = keep.tile([P, 8], F32)
+        minus_lam = keep.tile([P, PACK], F32)
+
+        for i in range(HALF):
+            statistics(0, i)
+        statistics(1, 0)
+        statistics(1, 1)
+        aggregate(0)
+        statistics(1, 2)
+        statistics(1, 3)
+        aggregate(1)
+        nc.scalar.copy(out=knots[:], in_=params[:, 0:KNOTS])
+        gain = keep.tile([P, FEATURES], F32)
+        shift = keep.tile([P, FEATURES], F32)
+        for n, dst in ((0, gain), (1, shift)):
+            nc.scalar.activation(
+                out=dst[:].rearrange("p (x m) -> p x m", m=4), func=ACT.Identity, scale=-1.0,
+                in_=params[:, PAD + n * FEATURES : PAD + (n + 1) * FEATURES].rearrange(
+                    "p (m x) -> p x m", m=4
+                ),
+            )
+
+        nc.vector.reciprocal(out=rstd[0][:], in_=rstd[0][:])
+        nc.vector.reciprocal(out=rstd[1][:], in_=rstd[1][:])
+        normalise(0)
+        nc.vector.tensor_sub(out=step, in0=knots[:, 1:12], in1=knots[:, 0:11])
+        nc.vector.tensor_sub(out=span2[:], in0=knots[:, 2:12], in1=knots[:, 0:10])
+        nc.vector.tensor_sub(out=span3[:], in0=knots[:, 3:12], in1=knots[:, 0:9])
+        apply_shift(0)
+        nc.vector.tensor_mul(out=part[:, 1, :], in0=step[:, 2:11], in1=span2[:, 1:10])
+        nc.vector.tensor_mul(out=part[:, 0, :], in0=step[:, 0:9], in1=span2[:, 0:9])
+        normalise(1)
+        nc.vector.tensor_mul(out=fall_den[:], in0=part[:, 1, :], in1=span3[:])
+        nc.scalar.activation(out=den[:, 9:18], in_=fall_den[:], func=ACT.Sqrt)
+        nc.vector.tensor_mul(out=den[:, 0:9], in0=part[:, 0, :], in1=span3[:])
+        nc.vector.tensor_sub(out=minus_span4[:], in0=knots[:, 0:8], in1=knots[:, 4:12])
+        apply_shift(1)
+        nc.vector.reciprocal(out=inv[:], in_=den[:])
+        nc.vector.tensor_mul(out=root_knot[:], in0=knots[:, 3:12], in1=root)
+        for n in VECTOR_SORTS:
+            sort_weights(n)
+
+        def rest_of_constants():
+            nc.vector.tensor_mul(out=minus_beta[:], in0=minus_span4[:], in1=inv_step[:, 3:11])
+            nc.vector.tensor_mul(out=lam[:, 3:9], in0=lam[:, 3:9], in1=fall_den[:, 0:6])
+            nc.vector.tensor_mul(out=minus_rho[:], in0=minus_span4[:], in1=inv_step[:, 0:8])
+            nc.vector.reciprocal(out=inv_lam[:], in_=lam[:, 0:8])
+            nc.vector.tensor_mul(out=minus_rho[:], in0=minus_rho[:], in1=lam[:, 1:9])
+            nc.vector.tensor_mul(out=minus_rho[:], in0=minus_rho[:], in1=inv_lam[:])
+
         basis = keep.tile([P, GROUPS * P, PACK], BF16, align_bytes=64)
         codes = keep.tile([P, GROUPS * P], U32, align_bytes=64)
         scales = keep.tile([P, GROUPS * P], U8, align_bytes=64)
@@ -213,14 +224,13 @@ def tile_fc_kanlayer_pb_s_kernel(tc, x, ln_w, ln_b, spline_weight, grid_bs, out)
             nc.tensor.matmul(dst, lhsT=lead, rhs=ident[:], is_transpose=True, start=True, stop=False)
             nc.tensor.matmul(dst, lhsT=trail, rhs=ident[:], is_transpose=True, start=False, stop=True)
 
-        order = (0, 1, 4, 5, 2, 6, 3, 7, 8, 9, 10, 11)
         cube = keep.tile([P, GROUPS, KNOTS, FEATURES], F32)
         trail_l = keep.tile([P, GROUPS, PACK, 2, FEATURES], F32)
         trail_r = keep.tile([P, GROUPS, PACK, 2, FEATURES], F32)
         left = keep.tile([P, PACK, GROUPS * P], BF16)
         right = {}
 
-        def square(j, groups=slice(0, GROUPS)):
+        def square(j, groups):
             at = cube[:, groups, slot(j), :]
             if j < PLAIN:
                 nc.scalar.activation(
@@ -232,25 +242,25 @@ def tile_fc_kanlayer_pb_s_kernel(tc, x, ln_w, ln_b, spline_weight, grid_bs, out)
                     scale=root[:, j - 3 : j - 2], bias=root_knot[:, j - 3 : j - 2],
                 )
 
-        def make_cube(j, groups=slice(0, GROUPS)):
+        def make_cube(j, groups):
             at = cube[:, groups, slot(j), :]
             nc.vector.scalar_tensor_tensor(
                 out=at, in0=minus_v[:, groups, :], scalar=knots[:, j : j + 1], in1=at,
                 op0=ALU.add, op1=ALU.mult,
             )
 
-        def make_trails(j):
-            at = cube[:, :, slot(j), :]
+        def make_trails(j, groups):
+            at = cube[:, groups, slot(j), :]
             g = j - 1
             if 0 <= g < FUNCS:
                 nc.vector.tensor_scalar(
-                    out=trail_l[:, :, g % PACK, g // PACK, :], in0=at,
+                    out=trail_l[:, groups, g % PACK, g // PACK, :], in0=at,
                     scalar1=minus_rho[:, g : g + 1], scalar2=0.0, op0=ALU.mult, op1=ALU.max,
                 )
             g = j - 3
             if 0 <= g < FUNCS:
                 nc.vector.tensor_scalar(
-                    out=trail_r[:, :, g % PACK, g // PACK, :], in0=at,
+                    out=trail_r[:, groups, g % PACK, g // PACK, :], in0=at,
                     scalar1=minus_beta[:, g : g + 1], scalar2=0.0, op0=ALU.mult, op1=ALU.min,
                 )
 
@@ -318,48 +328,41 @@ def tile_fc_kanlayer_pb_s_kernel(tc, x, ln_w, ln_b, spline_weight, grid_bs, out)
             nc.scalar.copy(out=out_sb[:, a, :], in_=acc[:])
             nc.sync.dma_start(out=out_rows[:, a, :], in_=out_sb[:, a, :])
 
-        LAST = len(order)
-        left_at = {3: 0, 5: 1, 7: 2, 8: 3}
-        right_at = {8: 0, 9: 1, 10: 2, 11: 3}
-        first, second = slice(0, HALF), slice(HALF, GROUPS)
-        square(order[0], first)
-        square(order[0], second)
-        for n in range(4):
-            sort_weights(n)
-        for k in range(1, 4):
-            square(order[k])
-        scale_of_left()
+        first, second, both = slice(0, HALF), slice(HALF, GROUPS), slice(0, GROUPS)
+        steps = [(j, half) for half in (first, second) for j in (0, 1, 4, 5)] + [(j, both) for j in (2, 6, 3, 7, 8)] + [(j, half) for half in (first, second) for j in (9, 10, 11)]
+        left_at = {3: [(0, 0)], 7: [(1, 0)], 9: [(0, 1)], 10: [(1, 1)], 11: [(0, 2)], 12: [(0, 3)], 16: [(1, 2)], 17: [(1, 3)]}
+        right_at = {12: 0, 13: 1, 14: 2, 15: 3}
+        for n in range(6):
+            square(*steps[n])
+            for s in {3: (2,), 5: (3,)}.get(n, ()):
+                sort_weights(s)
+        w_banks = [transpose_weights(half) for half in range(2)]
         pending = []
 
         def left_form(b, t):
             bank = left_bank(b, t)
             pending.append(lambda: copy_left(b, t, bank))
 
-        second_left_at = {6: 0, 7: 1, 20: 2, 21: 3}
-        for n in range(LAST + 1):
+        for n in range(len(steps) + 1):
+            if n < len(steps):
+                make_cube(*steps[n])
             if n == 0:
-                make_cube(order[0], first)
-                make_cube(order[0], second)
-            elif n < LAST:
-                make_cube(order[n])
-            if n + 4 < LAST:
-                square(order[n + 4])
+                rest_of_constants()
+                scale_of_left()
+            if n + 6 < len(steps):
+                square(*steps[n + 6])
+            if n in (4, 5):
+                group_weights((4, 5).index(n), w_banks[(4, 5).index(n)])
             for f in pending[:1]:
                 f()
             pending = pending[1:]
             if n:
-                k = n - 1
-                make_trails(order[k])
-                if k in left_at:
-                    left_form(0, left_at[k])
-                if k in right_at:
-                    for i in range(HALF):
-                        right_forms(i, right_at[k])
-            if n in second_left_at:
-                left_form(1, second_left_at[n])
-            if n in (5, 5+1):
-                w_t = transpose_weights(n - 5)
-                pending.append(lambda half=n - 5, w_t=w_t: group_weights(half, w_t))
+                make_trails(*steps[n - 1])
+                for b, t in left_at.get(n - 1, ()):
+                    left_form(b, t)
+                if n - 1 in right_at:
+                    for a in range(HALF):
+                        right_forms(a, right_at[n - 1])
         for f in pending:
             f()
         pending = []
@@ -367,12 +370,12 @@ def tile_fc_kanlayer_pb_s_kernel(tc, x, ln_w, ln_b, spline_weight, grid_bs, out)
         for a in range(GROUPS + 1):
             if a < GROUPS:
                 maximum(a)
+                for b, t in left_at.get(len(steps) + a, ()):
+                    left_form(b, t)
+                for f in pending:
+                    f()
+                pending = []
                 if a < HALF:
-                    if 20 + a in second_left_at:
-                        left_form(1, second_left_at[20 + a])
-                        for f in pending:
-                            f()
-                        pending = []
                     for t in range(PACK):
                         right_forms(a + HALF, t)
             if a:

@@ -23,6 +23,8 @@ GROUPS = 8
 HALF = 4
 KNOTS = 12
 PAD = 16
+BANK = 512
+QUAD = 32
 FUNCS = 8
 PLAIN = 3
 
@@ -49,14 +51,15 @@ def tile_fc_kanlayer_pb_s_kernel(tc, x, ln_w, ln_b, spline_weight, grid_bs, out)
 
         PARAMS = PAD + 2 * FEATURES
         row = keep.tile([P, PARAMS], BF16)
-        nc.vector.memset(row[:], 0.0)
-        nc.sync.dma_start(out=row[0:1, 0:KNOTS], in_=grid_bs.unsqueeze(0))
-        nc.sync.dma_start(out=row[0:1, PAD : PAD + FEATURES], in_=ln_w.unsqueeze(0))
-        nc.sync.dma_start(out=row[0:1, PAD + FEATURES : PARAMS], in_=ln_b.unsqueeze(0))
+        nc.vector.memset(row[QUAD : 2 * QUAD, :], 0.0)
+        nc.vector.memset(row[2 * QUAD : P, :], 0.0)
+        nc.sync.dma_start(out=row[0:QUAD, 0:KNOTS], in_=grid_bs.partition_broadcast(QUAD))
+        nc.sync.dma_start(out=row[0:QUAD, PAD : PAD + FEATURES], in_=ln_w.partition_broadcast(QUAD))
+        nc.sync.dma_start(out=row[0:QUAD, PAD + FEATURES : PARAMS], in_=ln_b.partition_broadcast(QUAD))
         w_sb = keep.tile([P, OUTS // P, K], BF16)
         nc.sync.dma_start(out=w_sb[:], in_=spline_weight.rearrange("(c q) k -> q c k", q=P))
         ones = keep.tile([P, P], BF16)
-        nc.vector.memset(ones[:], 1.0)
+        nc.vector.memset(ones[:], 1.0 / QUAD)
 
         ident = keep.tile([P, P], F32)
         make_identity(nc, ident[:])
@@ -77,7 +80,8 @@ def tile_fc_kanlayer_pb_s_kernel(tc, x, ln_w, ln_b, spline_weight, grid_bs, out)
         )
 
         params = psum.tile([P, PARAMS], F32, name="bank")
-        nc.tensor.matmul(params[:], lhsT=ones[:], rhs=row[:], start=True, stop=True)
+        for cols in (slice(0, KNOTS), slice(PAD, PARAMS)):
+            nc.tensor.matmul(params[:, cols], lhsT=ones[:], rhs=row[:, cols], start=True, stop=True)
         knots = keep.tile([P, KNOTS], F32)
         ctx.enter_context(
             tc.manual_schedule(
@@ -85,7 +89,6 @@ def tile_fc_kanlayer_pb_s_kernel(tc, x, ln_w, ln_b, spline_weight, grid_bs, out)
             )
         )
 
-        VECTOR_SORTS = (0, 1)
         w_words = w_sb[:].bitcast(F32)
         w_sorted = keep.tile([P, OUTS // P, 2, 2, FEATURES], F32)
         w_grouped = keep.tile([P, OUTS, PACK], BF16, align_bytes=64)
@@ -95,22 +98,19 @@ def tile_fc_kanlayer_pb_s_kernel(tc, x, ln_w, ln_b, spline_weight, grid_bs, out)
 
         def sort_weights(n):
             u, h = divmod(n, 2)
-            copy = nc.vector.tensor_copy if n in VECTOR_SORTS else nc.scalar.copy
-            copy(
+            nc.scalar.copy(
                 out=w_sorted[:, :, u, h, :].rearrange("p c (x m) -> p c x m", m=4),
                 in_=w_words[:, :, 2 * h + u : K // 2 : 4].rearrange("p c (m x) -> p c x m", m=4),
             )
 
-        def transpose_weights(half):
-            w_t = psum.tile([P, 2, 2 * P], F32, name="bank")
-            for c in range(2):
-                for u in range(2):
+        def transpose_weights(u):
+            for half in range(2):
+                for c in range(2):
                     nc.tensor.transpose(
-                        w_t[:, u, c * P : (c + 1) * P],
+                        w_banks[half][:, u, c * P : (c + 1) * P],
                         w_sorted[:, 2 * half + c, u, :, :].rearrange("p h q -> p (h q)"),
                         ident[:],
                     )
-            return w_t
 
         def group_weights(half, w_t):
             nc.scalar.copy(
@@ -135,9 +135,10 @@ def tile_fc_kanlayer_pb_s_kernel(tc, x, ln_w, ln_b, spline_weight, grid_bs, out)
         def statistics(b, i):
             nc.vector.bn_stats(out=stats[b][:, i, :], in_=x_sb[:, HALF * b + i, :])
 
-        def aggregate(b):
-            for i in range(HALF):
-                nc.vector.bn_aggr(out=mean_var[b][:, i, :], in_=stats[b][:, i, :])
+        def aggregate(b, i):
+            nc.vector.bn_aggr(out=mean_var[b][:, i, :], in_=stats[b][:, i, :])
+
+        def deviation(b):
             nc.scalar.activation(out=rstd[b][:], in_=mean_var[b][:, :, 1], func=ACT.Sqrt, bias=EPS)
 
         def normalise(b):
@@ -167,15 +168,6 @@ def tile_fc_kanlayer_pb_s_kernel(tc, x, ln_w, ln_b, spline_weight, grid_bs, out)
         inv_lam = keep.tile([P, 8], F32)
         minus_lam = keep.tile([P, PACK], F32)
 
-        for i in range(HALF):
-            statistics(0, i)
-        statistics(1, 0)
-        statistics(1, 1)
-        aggregate(0)
-        statistics(1, 2)
-        statistics(1, 3)
-        aggregate(1)
-        nc.scalar.copy(out=knots[:], in_=params[:, 0:KNOTS])
         gain = keep.tile([P, FEATURES], F32)
         shift = keep.tile([P, FEATURES], F32)
         for n, dst in ((0, gain), (1, shift)):
@@ -185,34 +177,51 @@ def tile_fc_kanlayer_pb_s_kernel(tc, x, ln_w, ln_b, spline_weight, grid_bs, out)
                     "p (m x) -> p x m", m=4
                 ),
             )
-
-        nc.vector.reciprocal(out=rstd[0][:], in_=rstd[0][:])
-        nc.vector.reciprocal(out=rstd[1][:], in_=rstd[1][:])
+        nc.scalar.copy(out=knots[:], in_=params[:, 0:KNOTS])
+        for i in range(HALF):
+            statistics(0, i)
+        statistics(1, 0)
+        statistics(1, 1)
+        for i in range(HALF):
+            aggregate(0, i)
+        deviation(0)
+        statistics(1, 2)
+        statistics(1, 3)
+        aggregate(1, 0)
+        aggregate(1, 1)
         normalise(0)
+        aggregate(1, 2)
+        aggregate(1, 3)
+        deviation(1)
         nc.vector.tensor_sub(out=step, in0=knots[:, 1:12], in1=knots[:, 0:11])
         nc.vector.tensor_sub(out=span2[:], in0=knots[:, 2:12], in1=knots[:, 0:10])
         nc.vector.tensor_sub(out=span3[:], in0=knots[:, 3:12], in1=knots[:, 0:9])
-        apply_shift(0)
+        nc.vector.reciprocal(out=rstd[0][:], in_=rstd[0][:])
+        normalise(1)
         nc.vector.tensor_mul(out=part[:, 1, :], in0=step[:, 2:11], in1=span2[:, 1:10])
         nc.vector.tensor_mul(out=part[:, 0, :], in0=step[:, 0:9], in1=span2[:, 0:9])
-        normalise(1)
+        nc.vector.reciprocal(out=rstd[1][:], in_=rstd[1][:])
+        apply_shift(0)
         nc.vector.tensor_mul(out=fall_den[:], in0=part[:, 1, :], in1=span3[:])
-        nc.scalar.activation(out=den[:, 9:18], in_=fall_den[:], func=ACT.Sqrt)
         nc.vector.tensor_mul(out=den[:, 0:9], in0=part[:, 0, :], in1=span3[:])
+        for n in (0,):
+            sort_weights(n)
+        nc.scalar.activation(out=den[:, 9:18], in_=fall_den[:], func=ACT.Sqrt)
         nc.vector.tensor_sub(out=minus_span4[:], in0=knots[:, 0:8], in1=knots[:, 4:12])
         apply_shift(1)
         nc.vector.reciprocal(out=inv[:], in_=den[:])
-        nc.vector.tensor_mul(out=root_knot[:], in0=knots[:, 3:12], in1=root)
-        for n in VECTOR_SORTS:
-            sort_weights(n)
 
-        def rest_of_constants():
-            nc.vector.tensor_mul(out=minus_beta[:], in0=minus_span4[:], in1=inv_step[:, 3:11])
-            nc.vector.tensor_mul(out=lam[:, 3:9], in0=lam[:, 3:9], in1=fall_den[:, 0:6])
-            nc.vector.tensor_mul(out=minus_rho[:], in0=minus_span4[:], in1=inv_step[:, 0:8])
-            nc.vector.reciprocal(out=inv_lam[:], in_=lam[:, 0:8])
-            nc.vector.tensor_mul(out=minus_rho[:], in0=minus_rho[:], in1=lam[:, 1:9])
-            nc.vector.tensor_mul(out=minus_rho[:], in0=minus_rho[:], in1=inv_lam[:])
+        def rest_of_constants(part_of):
+            if part_of == 0:
+                nc.vector.tensor_mul(out=root_knot[:], in0=knots[:, 3:12], in1=root)
+                nc.vector.tensor_mul(out=lam[:, 3:9], in0=lam[:, 3:9], in1=fall_den[:, 0:6])
+                nc.vector.tensor_mul(out=minus_beta[:], in0=minus_span4[:], in1=inv_step[:, 3:11])
+                nc.vector.tensor_mul(out=minus_rho[:], in0=minus_span4[:], in1=inv_step[:, 0:8])
+            elif part_of == 1:
+                nc.vector.reciprocal(out=inv_lam[:], in_=lam[:, 0:8])
+                nc.vector.tensor_mul(out=minus_rho[:], in0=minus_rho[:], in1=lam[:, 1:9])
+            elif part_of == 2:
+                nc.vector.tensor_mul(out=minus_rho[:], in0=minus_rho[:], in1=inv_lam[:])
 
         basis = keep.tile([P, GROUPS * P, PACK], BF16, align_bytes=64)
         codes = keep.tile([P, GROUPS * P], U32, align_bytes=64)
@@ -272,8 +281,15 @@ def tile_fc_kanlayer_pb_s_kernel(tc, x, ln_w, ln_b, spline_weight, grid_bs, out)
                     func=ACT.Identity, scale=-1.0,
                 )
 
+        def heat(dst, times, late=None):
+            for n in range(times):
+                nc.tensor.matmul(
+                    dst, lhsT=ident[:] if late is None else late, rhs=ident[:], start=True, stop=True
+                )
+
         def left_bank(b, t):
             bank = psum.tile([P, HALF * P], F32, name="bank")
+            heat(bank[:, 0:P], {}.get((b, t), 0))
             for i in range(HALF):
                 add_transposed(
                     bank[:, i * P : (i + 1) * P],
@@ -332,51 +348,71 @@ def tile_fc_kanlayer_pb_s_kernel(tc, x, ln_w, ln_b, spline_weight, grid_bs, out)
         steps = [(j, half) for half in (first, second) for j in (0, 1, 4, 5)] + [(j, both) for j in (2, 6, 3, 7, 8)] + [(j, half) for half in (first, second) for j in (9, 10, 11)]
         left_at = {3: [(0, 0)], 7: [(1, 0)], 9: [(0, 1)], 10: [(1, 1)], 11: [(0, 2)], 12: [(0, 3)], 16: [(1, 2)], 17: [(1, 3)]}
         right_at = {12: 0, 13: 1, 14: 2, 15: 3}
-        for n in range(6):
+        for n in range(2):
             square(*steps[n])
-            for s in {3: (2,), 5: (3,)}.get(n, ()):
-                sort_weights(s)
-        w_banks = [transpose_weights(half) for half in range(2)]
-        pending = []
+        for n in (1,):
+            sort_weights(n)
+        w_banks = [psum.tile([P, 2, 2 * P], F32, name="bank") for half in range(2)]
+        heat(w_banks[0][:, 0, 0:P], 0)
+        transpose_weights(0)
+        copies = []
 
         def left_form(b, t):
             bank = left_bank(b, t)
-            pending.append(lambda: copy_left(b, t, bank))
+            copies.append(lambda: copy_left(b, t, bank))
 
-        for n in range(len(steps) + 1):
-            if n < len(steps):
-                make_cube(*steps[n])
+        def trails_and_forms(n):
+            make_trails(*steps[n])
+            for b, t in left_at.get(n, ()):
+                left_form(b, t)
+            if n == 3:
+                transpose_weights(1)
+            for a in range(HALF):
+                if n in right_at:
+                    right_forms(a, right_at[n])
+
+        behind = []
+        for n in range(len(steps)):
+            make_cube(*steps[n])
+            width = (steps[n][1].stop - steps[n][1].start) * FEATURES
+            behind = [(s, columns + width) for s, columns in behind] + [(n, 0)]
+            rest_of_constants(n)
             if n == 0:
-                rest_of_constants()
+                for k in range(2, 6):
+                    square(*steps[k])
                 scale_of_left()
             if n + 6 < len(steps):
                 square(*steps[n + 6])
-            if n in (4, 5):
-                group_weights((4, 5).index(n), w_banks[(4, 5).index(n)])
-            for f in pending[:1]:
+            for s in {2: (2,), 4: (3,)}.get(n, ()):
+                sort_weights(s)
+            if n in (6, 7):
+                group_weights((6, 7).index(n), w_banks[(6, 7).index(n)])
+            for f in copies[:1]:
                 f()
-            pending = pending[1:]
-            if n:
-                make_trails(*steps[n - 1])
-                for b, t in left_at.get(n - 1, ()):
-                    left_form(b, t)
-                if n - 1 in right_at:
-                    for a in range(HALF):
-                        right_forms(a, right_at[n - 1])
-        for f in pending:
-            f()
-        pending = []
+            copies = copies[1:]
+            while behind and behind[0][1] >= BANK:
+                trails_and_forms(behind.pop(0)[0])
         quantise_weights()
-        for a in range(GROUPS + 1):
-            if a < GROUPS:
-                maximum(a)
-                for b, t in left_at.get(len(steps) + a, ()):
-                    left_form(b, t)
-                for f in pending:
-                    f()
-                pending = []
-                if a < HALF:
-                    for t in range(PACK):
-                        right_forms(a + HALF, t)
+        for s, columns in behind:
+            trails_and_forms(s)
+        for f in copies:
+            f()
+        copies = []
+        for a in range(GROUPS):
+            maximum(a)
+            for b, t in left_at.get(len(steps) + a, ()):
+                left_form(b, t)
+            for f in copies:
+                f()
+            copies = []
             if a:
-                store(a - 1, product(a - 1))
+                acc = product(a - 1)
+                if a < GROUPS - 1:
+                    store(a - 1, acc)
+            if a < HALF:
+                for t in range(PACK):
+                    right_forms(a + HALF, t)
+        last = product(GROUPS - 1)
+        nc.vector.tensor_copy(out=out_sb[:, GROUPS - 2, :], in_=acc[:])
+        nc.sync.dma_start(out=out_rows[:, GROUPS - 2, :], in_=out_sb[:, GROUPS - 2, :])
+        store(GROUPS - 1, last)

@@ -236,7 +236,7 @@ def tile_fc_kanlayer_pb_s_kernel(tc, x, ln_w, ln_b, spline_weight, grid_bs, out)
         cube = keep.tile([P, GROUPS, KNOTS, FEATURES], F32)
         trail_l = keep.tile([P, GROUPS, PACK, 2, FEATURES], F32)
         trail_r = keep.tile([P, GROUPS, PACK, 2, FEATURES], F32)
-        left = keep.tile([P, PACK, GROUPS * P], BF16)
+        left = [keep.tile([P, PACK, HALF * P], BF16, name="left%d" % b) for b in range(2)]
         right = {}
 
         def square(j, groups):
@@ -300,7 +300,7 @@ def tile_fc_kanlayer_pb_s_kernel(tc, x, ln_w, ln_b, spline_weight, grid_bs, out)
 
         def copy_left(b, t, bank):
             nc.scalar.activation(
-                out=left[:, t, HALF * P * b : HALF * P * (b + 1)], in_=bank[:], func=ACT.Relu,
+                out=left[b][:, t, :], in_=bank[:], func=ACT.Relu,
                 scale=minus_lam[:, t : t + 1],
             )
 
@@ -314,10 +314,11 @@ def tile_fc_kanlayer_pb_s_kernel(tc, x, ln_w, ln_b, spline_weight, grid_bs, out)
             )
 
         def maximum(a):
+            b, i = divmod(a, HALF)
             nc.vector.tensor_tensor(
-                out=basis[:, a * P : (a + 1) * P, :],
-                in0=right[a][:].rearrange("p t n -> p n t"),
-                in1=left[:, :, a * P : (a + 1) * P].rearrange("p t n -> p n t"),
+                out=basis[:, a * P : (a + 1) * P, :].rearrange("p (c i) t -> p c t i", i=PACK),
+                in0=right[a][:].rearrange("p t (c i) -> p c t i", i=PACK),
+                in1=left[b][:, :, i * P : (i + 1) * P].rearrange("p t (c i) -> p c t i", i=PACK),
                 op=ALU.max,
             )
 
@@ -345,7 +346,7 @@ def tile_fc_kanlayer_pb_s_kernel(tc, x, ln_w, ln_b, spline_weight, grid_bs, out)
             nc.sync.dma_start(out=out_rows[:, a, :], in_=out_sb[:, a, :])
 
         first, second, both = slice(0, HALF), slice(HALF, GROUPS), slice(0, GROUPS)
-        steps = [(j, half) for half in (first, second) for j in (0, 1, 4, 5)] + [(j, both) for j in (2, 6, 3, 7, 8)] + [(j, half) for half in (first, second) for j in (9, 10, 11)]
+        steps = [(j, half) for half in (first, second) for j in (0, 1, 4, 5)] + [(j, both) for j in (2, 6, 3, 7)] + [(j, half) for half in (first, second) for j in (8, 9, 10, 11)]
         left_at = {3: [(0, 0)], 7: [(1, 0)], 9: [(0, 1)], 10: [(1, 1)], 11: [(0, 2)], 12: [(0, 3)], 16: [(1, 2)], 17: [(1, 3)]}
         right_at = {12: 0, 13: 1, 14: 2, 15: 3}
         for n in range(2):

from contextlib import ExitStack

import concourse.mybir as mybir
from concourse.masks import make_identity

FLOPS = 2 * 1024 * 512 * 512

BF16 = mybir.dt.bfloat16
F32 = mybir.dt.float32
U32 = mybir.dt.uint32
U8 = mybir.dt.uint8
FP8X4 = mybir.dt.float8_e4m3fn_x4
ALU = mybir.AluOpType
ACT = mybir.ActivationFunctionType

P = 128
PACK = 4
FEATURES = 64
OUTS = 512
K = 512
EPS = 1e-5
GROUPS = 8
HALF = 4
KNOTS = 12
PAD = 16
BANK = 512
QUAD = 32
FUNCS = 8
PLAIN = 3


def slot(j):
    return 3 * (j % PACK) + j // PACK


def tile_fc_kanlayer_pb_s_kernel(tc, x, ln_w, ln_b, spline_weight, grid_bs, out):
    nc = tc.nc
    with ExitStack() as ctx:
        keep = ctx.enter_context(tc.tile_pool(name="keep", bufs=1))
        psum = ctx.enter_context(tc.psum_pool(name="psum", bufs=4))
        psum_right = ctx.enter_context(tc.psum_pool(name="psum_right", bufs=4))

        x_sb = keep.tile([P, GROUPS, FEATURES], BF16)
        nc.sync.dma_start(
            out=x_sb[:], in_=x.flatten_outer_dims().rearrange("(p a) d -> p a d", a=GROUPS)
        )
        one = keep.tile([P, 1], F32)
        nc.vector.memset(one[:], 1.0)
        warm = keep.tile([P, 1], F32)
        nc.scalar.activation(out=warm[:], in_=one[:], func=ACT.Sqrt)

        PARAMS = PAD + 2 * FEATURES
        row = keep.tile([P, PARAMS], BF16)
        nc.vector.memset(row[QUAD : 2 * QUAD, :], 0.0)
        nc.vector.memset(row[2 * QUAD : P, :], 0.0)
        nc.sync.dma_start(out=row[0:QUAD, 0:KNOTS], in_=grid_bs.partition_broadcast(QUAD))
        nc.sync.dma_start(out=row[0:QUAD, PAD : PAD + FEATURES], in_=ln_w.partition_broadcast(QUAD))
        nc.sync.dma_start(out=row[0:QUAD, PAD + FEATURES : PARAMS], in_=ln_b.partition_broadcast(QUAD))
        w_sb = keep.tile([P, OUTS // P, K], BF16)
        nc.sync.dma_start(out=w_sb[:], in_=spline_weight.rearrange("(c q) k -> q c k", q=P))
        ones = keep.tile([P, P], BF16)
        nc.vector.memset(ones[:], 1.0 / QUAD)

        ident = keep.tile([P, P], F32)
        make_identity(nc, ident[:])

        den = keep.tile([P, 29], F32)
        inv = keep.tile([P, 29], F32)
        fall_den = keep.tile([P, 9], F32)
        step = den[:, 18:29]
        span2 = keep.tile([P, 10], F32)
        span3 = keep.tile([P, 9], F32)
        minus_span4 = keep.tile([P, 8], F32)
        part = keep.tile([P, 2, 9], F32)

        ctx.enter_context(
            tc.manual_schedule(
                engines={mybir.EngineType.Activation, mybir.EngineType.PE, mybir.EngineType.DVE}
            )
        )

        params = psum.tile([P, PARAMS], F32, name="bank")
        for cols in (slice(0, KNOTS), slice(PAD, PARAMS)):
            nc.tensor.matmul(params[:, cols], lhsT=ones[:], rhs=row[:, cols], start=True, stop=True)
        knots = keep.tile([P, KNOTS], F32)
        ctx.enter_context(
            tc.manual_schedule(
                engines={mybir.EngineType.Activation, mybir.EngineType.PE, mybir.EngineType.DVE}
            )
        )

        w_words = w_sb[:].bitcast(F32)
        w_sorted = keep.tile([P, OUTS // P, 2, 2, FEATURES], F32)
        w_grouped = keep.tile([P, OUTS, PACK], BF16, align_bytes=64)
        w_grouped_words = w_grouped[:].bitcast(F32)
        w_codes = keep.tile([P, OUTS], U32, align_bytes=64)
        w_scales = keep.tile([P, OUTS], U8, align_bytes=64)

        def sort_weights(n):
            u, h = divmod(n, 2)
            nc.scalar.copy(
                out=w_sorted[:, :, u, h, :].rearrange("p c (x m) -> p c x m", m=4),
                in_=w_words[:, :, 2 * h + u : K // 2 : 4].rearrange("p c (m x) -> p c x m", m=4),
            )

        def transpose_weights(u):
            for half in range(2):
                for c in range(2):
                    nc.tensor.transpose(
                        w_banks[half][:, u, c * P : (c + 1) * P],
                        w_sorted[:, 2 * half + c, u, :, :].rearrange("p h q -> p (h q)"),
                        ident[:],
                    )

        def group_weights(half, w_t):
            nc.scalar.copy(
                out=w_grouped_words[:, 2 * P * half : 2 * P * (half + 1), :],
                in_=w_t[:].rearrange("p u o -> p o u"),
            )

        def quantise_weights():
            nc.vector.quantize_mx(
                out=w_codes[:].bitcast(FP8X4),
                scales=w_scales[:],
                in_=w_grouped[:].rearrange("p o t -> p (o t)"),
            )

        halves = range(2)
        stats = [keep.tile([P, HALF, 6], F32, name="stats%d" % b) for b in halves]
        mean_var = [keep.tile([P, HALF, 2], F32, name="mean_var%d" % b) for b in halves]
        rstd = [keep.tile([P, HALF], F32, name="rstd%d" % b) for b in halves]
        z = [keep.tile([P, HALF, FEATURES], F32, name="z%d" % b) for b in halves]
        minus_v = keep.tile([P, GROUPS, FEATURES], F32)

        def statistics(b, i):
            nc.vector.bn_stats(out=stats[b][:, i, :], in_=x_sb[:, HALF * b + i, :])

        def aggregate(b, i):
            nc.vector.bn_aggr(out=mean_var[b][:, i, :], in_=stats[b][:, i, :])

        def deviation(b):
            nc.scalar.activation(out=rstd[b][:], in_=mean_var[b][:, :, 1], func=ACT.Sqrt, bias=EPS)

        def normalise(b):
            for i in range(HALF):
                nc.vector.scalar_tensor_tensor(
                    out=z[b][:, i, :].rearrange("p (x m) -> p x m", m=4),
                    in0=x_sb[:, HALF * b + i, :].rearrange("p (m x) -> p x m", m=4),
                    scalar=mean_var[b][:, i, 0:1],
                    in1=gain[:].rearrange("p (x m) -> p x m", m=4),
                    op0=ALU.subtract,
                    op1=ALU.mult,
                )

        def apply_shift(b):
            for i in range(HALF):
                nc.vector.scalar_tensor_tensor(
                    out=minus_v[:, HALF * b + i, :], in0=z[b][:, i, :], scalar=rstd[b][:, i : i + 1],
                    in1=shift[:], op0=ALU.mult, op1=ALU.add,
                )

        root = inv[:, 9:18]
        inv_step = inv[:, 18:29]
        lam = inv[:, 0:9]
        root_knot = keep.tile([P, 9], F32)
        minus_beta = keep.tile([P, 8], F32)
        minus_rho = keep.tile([P, 8], F32)
        inv_lam = keep.tile([P, 8], F32)
        minus_lam = keep.tile([P, PACK], F32)

        gain = keep.tile([P, FEATURES], F32)
        shift = keep.tile([P, FEATURES], F32)
        for n, dst in ((0, gain), (1, shift)):
            nc.scalar.activation(
                out=dst[:].rearrange("p (x m) -> p x m", m=4), func=ACT.Identity, scale=-1.0,
                in_=params[:, PAD + n * FEATURES : PAD + (n + 1) * FEATURES].rearrange(
                    "p (m x) -> p x m", m=4
                ),
            )
        nc.scalar.copy(out=knots[:], in_=params[:, 0:KNOTS])
        for i in range(HALF):
            statistics(0, i)
        statistics(1, 0)
        statistics(1, 1)
        for i in range(HALF):
            aggregate(0, i)
        deviation(0)
        statistics(1, 2)
        statistics(1, 3)
        aggregate(1, 0)
        aggregate(1, 1)
        normalise(0)
        aggregate(1, 2)
        aggregate(1, 3)
        deviation(1)
        nc.vector.tensor_sub(out=step, in0=knots[:, 1:12], in1=knots[:, 0:11])
        nc.vector.tensor_sub(out=span2[:], in0=knots[:, 2:12], in1=knots[:, 0:10])
        nc.vector.tensor_sub(out=span3[:], in0=knots[:, 3:12], in1=knots[:, 0:9])
        nc.vector.reciprocal(out=rstd[0][:], in_=rstd[0][:])
        normalise(1)
        nc.vector.tensor_mul(out=part[:, 1, :], in0=step[:, 2:11], in1=span2[:, 1:10])
        nc.vector.tensor_mul(out=part[:, 0, :], in0=step[:, 0:9], in1=span2[:, 0:9])
        nc.vector.reciprocal(out=rstd[1][:], in_=rstd[1][:])
        apply_shift(0)
        nc.vector.tensor_mul(out=fall_den[:], in0=part[:, 1, :], in1=span3[:])
        nc.vector.tensor_mul(out=den[:, 0:9], in0=part[:, 0, :], in1=span3[:])
        for n in (0,):
            sort_weights(n)
        nc.scalar.activation(out=den[:, 9:18], in_=fall_den[:], func=ACT.Sqrt)
        nc.vector.tensor_sub(out=minus_span4[:], in0=knots[:, 0:8], in1=knots[:, 4:12])
        apply_shift(1)
        nc.vector.reciprocal(out=inv[:], in_=den[:])

        def rest_of_constants(part_of):
            if part_of == 0:
                nc.vector.tensor_mul(out=root_knot[:], in0=knots[:, 3:12], in1=root)
                nc.vector.tensor_mul(out=lam[:, 3:9], in0=lam[:, 3:9], in1=fall_den[:, 0:6])
                nc.vector.tensor_mul(out=minus_beta[:], in0=minus_span4[:], in1=inv_step[:, 3:11])
                nc.vector.tensor_mul(out=minus_rho[:], in0=minus_span4[:], in1=inv_step[:, 0:8])
            elif part_of == 1:
                nc.vector.reciprocal(out=inv_lam[:], in_=lam[:, 0:8])
                nc.vector.tensor_mul(out=minus_rho[:], in0=minus_rho[:], in1=lam[:, 1:9])
            elif part_of == 2:
                nc.vector.tensor_mul(out=minus_rho[:], in0=minus_rho[:], in1=inv_lam[:])

        basis = keep.tile([P, GROUPS * P, PACK], BF16, align_bytes=64)
        codes = keep.tile([P, GROUPS * P], U32, align_bytes=64)
        scales = keep.tile([P, GROUPS * P], U8, align_bytes=64)
        out_sb = keep.tile([P, GROUPS, OUTS], F32)
        out_rows = out.flatten_outer_dims().rearrange("(p a) o -> p a o", a=GROUPS)

        def add_transposed(dst, lead, trail):
            nc.tensor.matmul(dst, lhsT=lead, rhs=ident[:], is_transpose=True, start=True, stop=False)
            nc.tensor.matmul(dst, lhsT=trail, rhs=ident[:], is_transpose=True, start=False, stop=True)

        cube = keep.tile([P, GROUPS, KNOTS, FEATURES], F32)
        trail_l = keep.tile([P, GROUPS, PACK, 2, FEATURES], F32)
        trail_r = keep.tile([P, GROUPS, PACK, 2, FEATURES], F32)
        left = [keep.tile([P, PACK, HALF * P], BF16, name="left%d" % b) for b in range(2)]
        right = {}

        def square(j, groups):
            at = cube[:, groups, slot(j), :]
            if j < PLAIN:
                nc.scalar.activation(
                    out=at, in_=minus_v[:, groups, :], func=ACT.Square, bias=knots[:, j : j + 1]
                )
            else:
                nc.scalar.activation(
                    out=at, in_=minus_v[:, groups, :], func=ACT.Square,
                    scale=root[:, j - 3 : j - 2], bias=root_knot[:, j - 3 : j - 2],
                )

        def make_cube(j, groups):
            at = cube[:, groups, slot(j), :]
            nc.vector.scalar_tensor_tensor(
                out=at, in0=minus_v[:, groups, :], scalar=knots[:, j : j + 1], in1=at,
                op0=ALU.add, op1=ALU.mult,
            )

        def make_trails(j, groups):
            at = cube[:, groups, slot(j), :]
            g = j - 1
            if 0 <= g < FUNCS:
                nc.vector.tensor_scalar(
                    out=trail_l[:, groups, g % PACK, g // PACK, :], in0=at,
                    scalar1=minus_rho[:, g : g + 1], scalar2=0.0, op0=ALU.mult, op1=ALU.max,
                )
            g = j - 3
            if 0 <= g < FUNCS:
                nc.vector.tensor_scalar(
                    out=trail_r[:, groups, g % PACK, g // PACK, :], in0=at,
                    scalar1=minus_beta[:, g : g + 1], scalar2=0.0, op0=ALU.mult, op1=ALU.min,
                )

        def scale_of_left():
            for h in range(2):
                rows = slice(64 * h, 64 * h + 64)
                nc.scalar.activation(
                    out=minus_lam[rows, :], in_=lam[rows, PACK * h : PACK * h + PACK],
                    func=ACT.Identity, scale=-1.0,
                )

        def heat(dst, times, late=None):
            for n in range(times):
                nc.tensor.matmul(
                    dst, lhsT=ident[:] if late is None else late, rhs=ident[:], start=True, stop=True
                )

        def left_bank(b, t):
            bank = psum.tile([P, HALF * P], F32, name="bank")
            heat(bank[:, 0:P], {}.get((b, t), 0))
            for i in range(HALF):
                add_transposed(
                    bank[:, i * P : (i + 1) * P],
                    cube[:, HALF * b + i, slot(t) : slot(t) + 2, :].rearrange("p s q -> p (s q)"),
                    trail_l[:, HALF * b + i, t, :, :].rearrange("p h q -> p (h q)"),
                )
            return bank

        def copy_left(b, t, bank):
            nc.scalar.activation(
                out=left[b][:, t, :], in_=bank[:], func=ACT.Relu,
                scale=minus_lam[:, t : t + 1],
            )

        def right_forms(a, t):
            if a not in right:
                right[a] = psum_right.tile([P, PACK, P], F32, name="right")
            add_transposed(
                right[a][:, t, :],
                cube[:, a, slot(t) + 1 : slot(t) + 3, :].rearrange("p s q -> p (s q)"),
                trail_r[:, a, t, :, :].rearrange("p h q -> p (h q)"),
            )

        def maximum(a):
            b, i = divmod(a, HALF)
            nc.vector.tensor_tensor(
                out=basis[:, a * P : (a + 1) * P, :].rearrange("p (c i) t -> p c t i", i=PACK),
                in0=right[a][:].rearrange("p t (c i) -> p c t i", i=PACK),
                in1=left[b][:, :, i * P : (i + 1) * P].rearrange("p t (c i) -> p c t i", i=PACK),
                op=ALU.max,
            )

        def product(a):
            tokens = slice(a * P, (a + 1) * P)
            nc.vector.quantize_mx(
                out=codes[:, tokens].bitcast(FP8X4),
                scales=scales[:, tokens],
                in_=basis[:, tokens, :].rearrange("p n g -> p (n g)"),
            )
            acc = psum.tile([P, OUTS], F32, name="bank")
            nc.tensor.matmul_mx(
                out=acc[:],
                lhsT=codes[:, tokens].bitcast(FP8X4),
                lhsT_scale=scales[:, tokens],
                rhs=w_codes[:].bitcast(FP8X4),
                rhs_scale=w_scales[:],
                start=True,
                stop=True,
            )
            return acc

        def store(a, acc):
            nc.scalar.copy(out=out_sb[:, a, :], in_=acc[:])
            nc.sync.dma_start(out=out_rows[:, a, :], in_=out_sb[:, a, :])

        first, second, both = slice(0, HALF), slice(HALF, GROUPS), slice(0, GROUPS)
        steps = [(j, half) for half in (first, second) for j in (0, 1, 4, 5)] + [(j, both) for j in (2, 6, 3, 7)] + [(j, half) for half in (first, second) for j in (8, 9, 10, 11)]
        left_at = {3: [(0, 0)], 7: [(1, 0)], 9: [(0, 1)], 10: [(1, 1)], 11: [(0, 2)], 12: [(0, 3)], 16: [(1, 2)], 17: [(1, 3)]}
        right_at = {12: 0, 13: 1, 14: 2, 15: 3}
        for n in range(2):
            square(*steps[n])
        for n in (1,):
            sort_weights(n)
        w_banks = [psum.tile([P, 2, 2 * P], F32, name="bank") for half in range(2)]
        heat(w_banks[0][:, 0, 0:P], 0)
        transpose_weights(0)
        copies = []

        def left_form(b, t):
            bank = left_bank(b, t)
            copies.append(lambda: copy_left(b, t, bank))

        def trails_and_forms(n):
            make_trails(*steps[n])
            for b, t in left_at.get(n, ()):
                left_form(b, t)
            if n == 3:
                transpose_weights(1)
            for a in range(HALF):
                if n in right_at:
                    right_forms(a, right_at[n])

        behind = []
        for n in range(len(steps)):
            make_cube(*steps[n])
            width = (steps[n][1].stop - steps[n][1].start) * FEATURES
            behind = [(s, columns + width) for s, columns in behind] + [(n, 0)]
            rest_of_constants(n)
            if n == 0:
                for k in range(2, 6):
                    square(*steps[k])
                scale_of_left()
            if n + 6 < len(steps):
                square(*steps[n + 6])
            for s in {2: (2,), 4: (3,)}.get(n, ()):
                sort_weights(s)
            if n in (6, 7):
                group_weights((6, 7).index(n), w_banks[(6, 7).index(n)])
            for f in copies[:1]:
                f()
            copies = copies[1:]
            while behind and behind[0][1] >= BANK:
                trails_and_forms(behind.pop(0)[0])
        quantise_weights()
        for s, columns in behind:
            trails_and_forms(s)
        for f in copies:
            f()
        copies = []
        for a in range(GROUPS):
            maximum(a)
            for b, t in left_at.get(len(steps) + a, ()):
                left_form(b, t)
            for f in copies:
                f()
            copies = []
            if a:
                acc = product(a - 1)
                if a < GROUPS - 1:
                    store(a - 1, acc)
            if a < HALF:
                for t in range(PACK):
                    right_forms(a + HALF, t)
        last = product(GROUPS - 1)
        nc.vector.tensor_copy(out=out_sb[:, GROUPS - 2, :], in_=acc[:])
        nc.sync.dma_start(out=out_rows[:, GROUPS - 2, :], in_=out_sb[:, GROUPS - 2, :])
        store(GROUPS - 1, last)
